import numpy as np
import ml_dtypes


def mxq(x, axis, fmt="e4m3"):
    dtype, down = {"e4m3": (ml_dtypes.float8_e4m3fn, 7), "e5m2": (ml_dtypes.float8_e5m2, 14)}[fmt]
    v = np.moveaxis(np.asarray(x, np.float32).astype(ml_dtypes.bfloat16).astype(np.float64), axis, -1)
    blocks = v.reshape(v.shape[:-1] + (-1, 32))
    amax = np.abs(blocks).max(-1, keepdims=True)
    byte = np.maximum(np.where(amax > 0, np.frexp(amax)[1] - 1 + 127, 0) - down, 1)
    scale = np.exp2(byte - 127.0)
    codes = (blocks / scale).astype(np.float32).astype(dtype).astype(np.float64)
    return np.moveaxis((codes * scale).reshape(v.shape), -1, axis)


WIDE = False


def mx_kscale(k):
    if not WIDE:
        return np.ones(k)
    levels = np.array([10, -10, 5, -5, 0])
    a = np.random.permutation(np.resize(levels, k // 512 * 4)).reshape(k // 512, 4)
    idx = np.arange(k)
    return np.exp2(a[idx // 512, idx % 128 // 32])


BF16 = ml_dtypes.bfloat16


def bf(x):
    return np.asarray(x, np.float32).astype(BF16)


def f64(x):
    return np.asarray(x).astype(np.float64)


T, BLK, B, NH, NW, C, K = 16, 4, 4, 8, 8, 512, 1024
R = B * NH * NW
HAD = np.array([[1.0, 1.0, 1.0, 1.0],
                [1.0, -1.0, 1.0, -1.0],
                [1.0, 1.0, -1.0, -1.0],
                [1.0, -1.0, -1.0, 1.0]])


def setup_inputs():
    s = mx_kscale(C)
    return {"trans": bf(np.random.standard_normal((T, B, NH, NW, C)) * s),
            "weight": bf(np.random.standard_normal((T, C, K)) * 2.0 / np.sqrt(C) / s[None, :, None]),
            "bias": bf(np.random.standard_normal((1, 1, 1, K)) * 0.2)}


def reference(trans, weight, bias):
    mixed = mxq(f64(trans).reshape(T, R, C), 2, "e4m3") @ mxq(f64(weight), 1, "e4m3")
    mixed = mixed.reshape(BLK, BLK, B, NH, NW, K)
    out = np.zeros((B, NH, BLK, NW, BLK, K))
    for i in range(BLK):
        for j in range(BLK):
            acc = np.zeros((B, NH, NW, K))
            for u in range(BLK):
                for v in range(BLK):
                    acc = acc + HAD[i, u] * HAD[j, v] * mixed[u, v]
            out[:, :, i, :, j, :] = acc
    out = out * (1.0 / T)
    return out.reshape(B, NH * BLK, NW * BLK, K) + f64(bias)

@@ -1,0 +1,187 @@
+from contextlib import ExitStack
+
+import concourse.mybir as mybir
+from concourse.masks import make_identity
+
+FP8X4 = mybir.dt.float8_e4m3fn_x4
+BF16 = mybir.dt.bfloat16
+F32 = mybir.dt.float32
+U32 = mybir.dt.uint32
+U8 = mybir.dt.uint8
+ALU = mybir.AluOpType
+ACT = mybir.ActivationFunctionType
+
+P = 128
+T = 16
+C = 512
+K = 1024
+NH = 512
+FLOPS = 2 * 16 * 256 * 512 * 1024
+
+H4 = ((1, 1, 1, 1), (1, -1, 1, -1), (1, 1, -1, -1), (1, -1, -1, 1))
+SCALE = 1.0 / 16.0
+
+R_ON_VECTOR = ((0, 1), (0, 3))
+
+
+def tile_iwht2layer_pa_t_kernel(tc, trans, weight, bias, out):
+    nc = tc.nc
+    with ExitStack() as ctx:
+        const = ctx.enter_context(tc.tile_pool(name="const", bufs=1))
+        xraw = ctx.enter_context(tc.tile_pool(name="xraw", bufs=6))
+        tgrp = ctx.enter_context(tc.tile_pool(name="tgrp", bufs=3))
+        wraw = ctx.enter_context(tc.tile_pool(name="wraw", bufs=6))
+        wgrp = ctx.enter_context(tc.tile_pool(name="wgrp", bufs=3))
+        wcod = ctx.enter_context(tc.tile_pool(name="wcod", bufs=3))
+        xpool = ctx.enter_context(tc.tile_pool(name="xpool", bufs=12))
+        psum = ctx.enter_context(tc.psum_pool(name="psum", bufs=8))
+
+        ident = const.tile([P, P], F32, name="ident")
+        make_identity(nc, ident[:])
+        bias_bc = const.tile([P, K], BF16, name="bias_bc")
+        tcod = const.tile([P, T, 512], U32, align_bytes=64, name="tcod")
+        tsc = const.tile([P, T, 512], U8, align_bytes=64, name="tsc")
+
+        xr_of = {}
+        wr_of = {}
+        wc_of = {}
+        x_of = {}
+
+        def load_x(t):
+            xr = xraw.tile([P, 2 * C], BF16, name="xr")
+            nc.sync.dma_start(
+                out=xr[:].rearrange("p (a c) -> p a c", a=2),
+                in_=trans[t].rearrange("b h w c -> (b h w) c").rearrange("(a p) c -> p a c", p=P),
+            )
+            xr_of[t] = xr
+
+        def load_w(nt, t):
+            wr = wraw.tile([P, 4 * NH], BF16, name="wr")
+            nc.sync.dma_start(
+                out=wr[:].rearrange("p (j n) -> p j n", j=4),
+                in_=weight[t].rearrange("(p j) n -> p j n", j=4)[:, :, nt * NH : (nt + 1) * NH],
+            )
+            wr_of[(nt, t)] = wr
+
+        def prep_x(t):
+            xr = xr_of[t]
+            words = xr[:].bitcast(F32).rearrange("p (a w u) -> p a w u", a=2, u=2)
+            xt = psum.tile([P, NH], F32, tag="bank", name="xt")
+            for a in range(2):
+                for u in range(2):
+                    q = 2 * a + u
+                    nc.tensor.transpose(xt[:, q * P : (q + 1) * P], words[:, a, :, u], ident[:])
+            tg = tgrp.tile([P, 2048], BF16, align_bytes=64, name="tg")
+            nc.scalar.copy(
+                out=tg[:, 0:1024].bitcast(F32).rearrange("p (a r u) -> p a r u", a=2, u=2),
+                in_=xt[:].rearrange("p (a u r) -> p a r u", a=2, u=2),
+            )
+            if t % 4 == 0:
+                nc.vector.quantize_mx(
+                    out=tcod[:, t, 0:256].bitcast(FP8X4), scales=tsc[:, t, 0:256], in_=tg[:, 0:1024]
+                )
+            else:
+                nc.vector.tensor_scalar_mul(out=tg[:, 1024:2048], in0=tg[:, 0:1024], scalar1=-1.0)
+                nc.vector.quantize_mx(out=tcod[:, t, :].bitcast(FP8X4), scales=tsc[:, t, :], in_=tg[:])
+
+        def prep_w(nt, t):
+            u, v = divmod(t, 4)
+            if v == 0:
+                wc = wcod.tile([P, 4, NH], U32, align_bytes=64, name="wc")
+                ws = wcod.tile([P, 4, NH], U8, align_bytes=64, name="ws")
+                wc_of[(nt, u)] = (wc, ws)
+            wc, ws = wc_of[(nt, u)]
+            wr = wr_of[(nt, t)]
+            wg = wgrp.tile([P, 4 * NH], BF16, align_bytes=64, name="wg")
+            dst = wg[:].rearrange("p (c i t) -> p c t i", i=4, t=4)
+            src = wr[:].rearrange("p (t c i) -> p c t i", t=4, i=4)
+            if (nt, t) in R_ON_VECTOR:
+                nc.vector.tensor_copy(out=dst, in_=src)
+            else:
+                nc.scalar.copy(out=dst, in_=src)
+            nc.vector.quantize_mx(out=wc[:, v, :].bitcast(FP8X4), scales=ws[:, v, :], in_=wg[:])
+
+        def store(nt, rt, i, xt):
+            view = out[2 * rt : 2 * rt + 2, :, :, nt * NH : (nt + 1) * NH]
+            view = view.rearrange("b (h i) (w j) k -> i j (b h) w k", i=4, j=4)
+            for j in range(4):
+                nc.sync.dma_start(out=view[i, j], in_=xt[:, j, :])
+
+        def butterfly(bank, lo, hi, j):
+            nc.vector.scalar_tensor_tensor(
+                out=hi[:, j, :], in0=bank[:], scalar=-SCALE, in1=lo[:, j, :], op0=ALU.mult, op1=ALU.add
+            )
+            nc.vector.scalar_tensor_tensor(
+                out=lo[:, j, :], in0=bank[:], scalar=SCALE, in1=lo[:, j, :], op0=ALU.mult, op1=ALU.add
+            )
+
+        def mx_round(nt, u):
+            wc, ws = wc_of[(nt, u)]
+            for rt in range(2):
+                xn = xpool.tile([P, 4, NH], F32, tag="x", name="xn")
+                x_of[(nt, rt, u)] = xn
+                for j in range(4):
+                    bank = psum.tile([P, NH], F32, tag="bank", name="bank")
+                    for v in range(4):
+                        t = 4 * u + v
+                        col = (0 if H4[j][v] > 0 else 256) + rt * P
+                        nc.tensor.matmul_mx(
+                            out=bank[:],
+                            lhsT=tcod[:, t, col : col + P].bitcast(FP8X4),
+                            lhsT_scale=tsc[:, t, col : col + P],
+                            rhs=wc[:, v, :].bitcast(FP8X4),
+                            rhs_scale=ws[:, v, :],
+                            start=(v == 0),
+                            stop=(v == 3),
+                        )
+                    if u == 0:
+                        nc.vector.scalar_tensor_tensor(
+                            out=xn[:, j, :],
+                            in0=bank[:],
+                            scalar=SCALE,
+                            in1=bias_bc[:, nt * NH : (nt + 1) * NH],
+                            op0=ALU.mult,
+                            op1=ALU.add,
+                        )
+                    elif u == 2:
+                        nc.scalar.activation(out=xn[:, j, :], in_=bank[:], func=ACT.Copy, scale=SCALE)
+                    else:
+                        butterfly(bank, x_of[(nt, rt, u - 1)], xn, j)
+                if u == 3:
+                    for e in range(2):
+                        lo = x_of[(nt, rt, e)]
+                        hi = x_of[(nt, rt, 2 + e)]
+                        yd = xpool.tile([P, 4, NH], F32, tag="x", name="yd")
+                        nc.vector.tensor_tensor(out=yd[:], in0=lo[:], in1=hi[:], op=ALU.subtract)
+                        store(nt, rt, 2 + e, yd)
+                        nc.vector.tensor_tensor(out=lo[:], in0=lo[:], in1=hi[:], op=ALU.add)
+                        store(nt, rt, e, lo)
+
+        rounds = [(nt, u) for nt in range(2) for u in range(4)]
+        for t in range(4):
+            load_x(t)
+        for t in range(4):
+            load_w(0, t)
+        for t in range(4, 8):
+            load_x(t)
+        nc.sync.dma_start(out=bias_bc[:], in_=bias.rearrange("a b c k -> (a b c k)").partition_broadcast(P))
+        for t in range(4):
+            prep_x(t)
+        for t in range(4):
+            prep_w(0, t)
+        for k in range(8):
+            nt, u = rounds[k]
+            if k + 1 < 8:
+                nnt, nu = rounds[k + 1]
+                for v in range(4):
+                    load_w(nnt, 4 * nu + v)
+            if k + 2 < 4:
+                for v in range(4):
+                    load_x(4 * (k + 2) + v)
+            if k + 1 < 4:
+                for v in range(4):
+                    prep_x(4 * (k + 1) + v)
+            if k + 1 < 8:
+                for v in range(4):
+                    prep_w(nnt, 4 * nu + v)
+            mx_round(nt, u)

@@ -22,6 +22,9 @@ H4 = ((1, 1, 1, 1), (1, -1, 1, -1), (1, 1, -1, -1), (1, -1, -1, 1))
 SCALE = 1.0 / 16.0
 
 R_ON_VECTOR = ((0, 1), (0, 3))
+R8_HALVES = ()
+B_ON_GPSIMD = ((0, 0, 0), (0, 0, 1), (0, 1, 0), (0, 1, 1))
+LOOKAHEAD = 1
 
 
 def tile_iwht2layer_pa_t_kernel(tc, trans, weight, bias, out):
@@ -33,7 +36,8 @@ def tile_iwht2layer_pa_t_kernel(tc, trans, weight, bias, out):
         wraw = ctx.enter_context(tc.tile_pool(name="wraw", bufs=6))
         wgrp = ctx.enter_context(tc.tile_pool(name="wgrp", bufs=3))
         wcod = ctx.enter_context(tc.tile_pool(name="wcod", bufs=3))
-        xpool = ctx.enter_context(tc.tile_pool(name="xpool", bufs=12))
+        xpool = ctx.enter_context(tc.tile_pool(name="xpool", bufs=10))
+        ypool = ctx.enter_context(tc.tile_pool(name="ypool", bufs=8))
         psum = ctx.enter_context(tc.psum_pool(name="psum", bufs=8))
 
         ident = const.tile([P, P], F32, name="ident")
@@ -46,6 +50,7 @@ def tile_iwht2layer_pa_t_kernel(tc, trans, weight, bias, out):
         wr_of = {}
         wc_of = {}
         x_of = {}
+        open_banks = {}
 
         def load_x(t):
             xr = xraw.tile([P, 2 * C], BF16, name="xr")
@@ -76,7 +81,7 @@ def tile_iwht2layer_pa_t_kernel(tc, trans, weight, bias, out):
                 out=tg[:, 0:1024].bitcast(F32).rearrange("p (a r u) -> p a r u", a=2, u=2),
                 in_=xt[:].rearrange("p (a u r) -> p a r u", a=2, u=2),
             )
-            if t % 4 == 0:
+            if t % 4 == 0 and not (t == 12 and len(R8_HALVES) > 0):
                 nc.vector.quantize_mx(
                     out=tcod[:, t, 0:256].bitcast(FP8X4), scales=tsc[:, t, 0:256], in_=tg[:, 0:1024]
                 )
@@ -101,39 +106,41 @@ def tile_iwht2layer_pa_t_kernel(tc, trans, weight, bias, out):
                 nc.scalar.copy(out=dst, in_=src)
             nc.vector.quantize_mx(out=wc[:, v, :].bitcast(FP8X4), scales=ws[:, v, :], in_=wg[:])
 
-        def store(nt, rt, i, xt):
+        def store(nt, rt, i, j, ap):
             view = out[2 * rt : 2 * rt + 2, :, :, nt * NH : (nt + 1) * NH]
             view = view.rearrange("b (h i) (w j) k -> i j (b h) w k", i=4, j=4)
-            for j in range(4):
-                nc.sync.dma_start(out=view[i, j], in_=xt[:, j, :])
+            nc.sync.dma_start(out=view[i, j], in_=ap)
 
-        def butterfly(bank, lo, hi, j):
+        def butterfly(bank, lo, hi):
             nc.vector.scalar_tensor_tensor(
-                out=hi[:, j, :], in0=bank[:], scalar=-SCALE, in1=lo[:, j, :], op0=ALU.mult, op1=ALU.add
+                out=hi, in0=bank[:], scalar=-SCALE, in1=lo, op0=ALU.mult, op1=ALU.add
             )
             nc.vector.scalar_tensor_tensor(
-                out=lo[:, j, :], in0=bank[:], scalar=SCALE, in1=lo[:, j, :], op0=ALU.mult, op1=ALU.add
+                out=lo, in0=bank[:], scalar=SCALE, in1=lo, op0=ALU.mult, op1=ALU.add
             )
+
+        def passes(bank, nt, u, rt, j, flip, start, stop):
+            wc, ws = wc_of[(nt, u)]
+            for v in range(4):
+                t = 4 * u + v
+                col = (0 if H4[j][v] * flip > 0 else 256) + rt * P
+                nc.tensor.matmul_mx(
+                    out=bank[:],
+                    lhsT=tcod[:, t, col : col + P].bitcast(FP8X4),
+                    lhsT_scale=tsc[:, t, col : col + P],
+                    rhs=wc[:, v, :].bitcast(FP8X4),
+                    rhs_scale=ws[:, v, :],
+                    start=(start and v == 0),
+                    stop=(stop and v == 3),
+                )
 
         def mx_round(nt, u):
-            wc, ws = wc_of[(nt, u)]
             for rt in range(2):
                 xn = xpool.tile([P, 4, NH], F32, tag="x", name="xn")
                 x_of[(nt, rt, u)] = xn
                 for j in range(4):
                     bank = psum.tile([P, NH], F32, tag="bank", name="bank")
-                    for v in range(4):
-                        t = 4 * u + v
-                        col = (0 if H4[j][v] > 0 else 256) + rt * P
-                        nc.tensor.matmul_mx(
-                            out=bank[:],
-                            lhsT=tcod[:, t, col : col + P].bitcast(FP8X4),
-                            lhsT_scale=tsc[:, t, col : col + P],
-                            rhs=wc[:, v, :].bitcast(FP8X4),
-                            rhs_scale=ws[:, v, :],
-                            start=(v == 0),
-                            stop=(v == 3),
-                        )
+                    passes(bank, nt, u, rt, j, 1, True, True)
                     if u == 0:
                         nc.vector.scalar_tensor_tensor(
                             out=xn[:, j, :],
@@ -146,42 +153,86 @@ def tile_iwht2layer_pa_t_kernel(tc, trans, weight, bias, out):
                     elif u == 2:
                         nc.scalar.activation(out=xn[:, j, :], in_=bank[:], func=ACT.Copy, scale=SCALE)
                     else:
-                        butterfly(bank, x_of[(nt, rt, u - 1)], xn, j)
+                        butterfly(bank, x_of[(nt, rt, u - 1)][:, j, :], xn[:, j, :])
                 if u == 3:
                     for e in range(2):
                         lo = x_of[(nt, rt, e)]
                         hi = x_of[(nt, rt, 2 + e)]
-                        yd = xpool.tile([P, 4, NH], F32, tag="x", name="yd")
-                        nc.vector.tensor_tensor(out=yd[:], in0=lo[:], in1=hi[:], op=ALU.subtract)
-                        store(nt, rt, 2 + e, yd)
-                        nc.vector.tensor_tensor(out=lo[:], in0=lo[:], in1=hi[:], op=ALU.add)
-                        store(nt, rt, e, lo)
+                        if (nt, rt, e) in B_ON_GPSIMD:
+                            for j in range(4):
+                                ys = ypool.tile([P, NH], F32, name="ys")
+                                nc.gpsimd.tensor_tensor(out=ys[:], in0=lo[:, j, :], in1=hi[:, j, :], op=ALU.subtract)
+                                store(nt, rt, 2 + e, j, ys[:])
+                                nc.gpsimd.tensor_tensor(out=lo[:, j, :], in0=lo[:, j, :], in1=hi[:, j, :], op=ALU.add)
+                                store(nt, rt, e, j, lo[:, j, :])
+                        else:
+                            nc.vector.tensor_tensor(out=hi[:], in0=lo[:], in1=hi[:], op=ALU.subtract)
+                            for j in range(4):
+                                store(nt, rt, 2 + e, j, hi[:, j, :])
+                            nc.vector.scalar_tensor_tensor(
+                                out=lo[:], in0=lo[:], scalar=2.0, in1=hi[:], op0=ALU.mult, op1=ALU.subtract
+                            )
+                            for j in range(4):
+                                store(nt, rt, e, j, lo[:, j, :])
+
+        def r8_open(nt, rt):
+            for e in range(2):
+                for j in range(4):
+                    bank = psum.tile([P, NH], F32, tag="bank", name="bank")
+                    open_banks[(e, j)] = bank
+                    passes(bank, nt, 2, rt, j, 1, True, False)
+
+        def r8_close(nt, rt, e, j, bank):
+            passes(bank, nt, 3, rt, j, 1 - 2 * e, False, True)
+            lo = x_of[(nt, rt, e)]
+            ys = ypool.tile([P, NH], F32, name="ys")
+            butterfly(bank, lo[:, j, :], ys[:])
+            store(nt, rt, 2 + e, j, ys[:])
+            store(nt, rt, e, j, lo[:, j, :])
+
+        def r8_finish(nt):
+            for e in range(2):
+                for j in range(4):
+                    r8_close(nt, 0, e, j, open_banks[(e, j)])
+            for e in range(2):
+                for j in range(4):
+                    bank = psum.tile([P, NH], F32, tag="bank", name="bank")
+                    passes(bank, nt, 2, 1, j, 1, True, False)
+                    r8_close(nt, 1, e, j, bank)
 
         rounds = [(nt, u) for nt in range(2) for u in range(4)]
-        for t in range(4):
-            load_x(t)
-        for t in range(4):
-            load_w(0, t)
-        for t in range(4, 8):
-            load_x(t)
-        nc.sync.dma_start(out=bias_bc[:], in_=bias.rearrange("a b c k -> (a b c k)").partition_broadcast(P))
-        for t in range(4):
-            prep_x(t)
-        for t in range(4):
-            prep_w(0, t)
+
+        def loads(k):
+            if k < 4:
+                for v in range(4):
+                    load_x(4 * k + v)
+            if k == 1:
+                nc.sync.dma_start(
+                    out=bias_bc[:], in_=bias.rearrange("a b c k -> (a b c k)").partition_broadcast(P)
+                )
+            if k < 8:
+                for v in range(4):
+                    load_w(rounds[k][0], 4 * rounds[k][1] + v)
+
+        def prep(k):
+            if k < 4:
+                for v in range(4):
+                    prep_x(4 * k + v)
+            if k < 8:
+                for v in range(4):
+                    prep_w(rounds[k][0], 4 * rounds[k][1] + v)
+
+        for k in range(LOOKAHEAD + 1):
+            loads(k)
+        for k in range(LOOKAHEAD):
+            prep(k)
         for k in range(8):
             nt, u = rounds[k]
-            if k + 1 < 8:
-                nnt, nu = rounds[k + 1]
-                for v in range(4):
-                    load_w(nnt, 4 * nu + v)
-            if k + 2 < 4:
-                for v in range(4):
-                    load_x(4 * (k + 2) + v)
-            if k + 1 < 4:
-                for v in range(4):
-                    prep_x(4 * (k + 1) + v)
-            if k + 1 < 8:
-                for v in range(4):
-                    prep_w(nnt, 4 * nu + v)
-            mx_round(nt, u)
+            loads(k + LOOKAHEAD + 1)
+            prep(k + LOOKAHEAD)
+            if nt in R8_HALVES and u == 2:
+                r8_open(nt, 0)
+            elif nt in R8_HALVES and u == 3:
+                r8_finish(nt)
+            else:
+                mx_round(nt, u)

@@ -21,31 +21,37 @@ FLOPS = 2 * 16 * 256 * 512 * 1024
 H4 = ((1, 1, 1, 1), (1, -1, 1, -1), (1, 1, -1, -1), (1, -1, -1, 1))
 SCALE = 1.0 / 16.0
 
-R_ON_VECTOR = ((0, 1), (0, 3))
+R_ON_VECTOR = ((0, 1), (0, 3), (0, 9), (1, 3), (1, 9))
 R8_HALVES = ()
-B_ON_GPSIMD = ((0, 0, 0), (0, 0, 1), (0, 1, 0), (0, 1, 1))
+B_ON_GPSIMD = ((0, 0, 0), (0, 0, 1), (0, 1, 0), (0, 1, 1), (1, 0, 1))
 LOOKAHEAD = 1
+G_DRAIN = (0, 0, 0, 4, 4, 4, 4, 0)
 
 
 def tile_iwht2layer_pa_t_kernel(tc, trans, weight, bias, out):
     nc = tc.nc
     with ExitStack() as ctx:
         const = ctx.enter_context(tc.tile_pool(name="const", bufs=1))
-        xraw = ctx.enter_context(tc.tile_pool(name="xraw", bufs=6))
-        tgrp = ctx.enter_context(tc.tile_pool(name="tgrp", bufs=3))
         wraw = ctx.enter_context(tc.tile_pool(name="wraw", bufs=6))
         wgrp = ctx.enter_context(tc.tile_pool(name="wgrp", bufs=3))
         wcod = ctx.enter_context(tc.tile_pool(name="wcod", bufs=3))
-        xpool = ctx.enter_context(tc.tile_pool(name="xpool", bufs=10))
-        ypool = ctx.enter_context(tc.tile_pool(name="ypool", bufs=8))
+        xpool = ctx.enter_context(tc.tile_pool(name="xpool", bufs=9))
+        ypool = ctx.enter_context(tc.tile_pool(name="ypool", bufs=6))
         psum = ctx.enter_context(tc.psum_pool(name="psum", bufs=8))
 
         ident = const.tile([P, P], F32, name="ident")
         make_identity(nc, ident[:])
-        bias_bc = const.tile([P, K], BF16, name="bias_bc")
+        bias_bc = const.tile([P, K], F32, name="bias_bc")
+        ones = const.tile([P, P], BF16, name="ones")
+        brow = const.tile([P, K], BF16, name="brow")
+        nc.vector.memset(ones[:], 1.0)
+        nc.vector.memset(brow[:], 0.0)
         tcod = const.tile([P, T, 512], U32, align_bytes=64, name="tcod")
         tsc = const.tile([P, T, 512], U8, align_bytes=64, name="tsc")
 
+        late = {}
+        g_todo = []
+        st_todo = []
         xr_of = {}
         wr_of = {}
         wc_of = {}
@@ -53,7 +59,7 @@ def tile_iwht2layer_pa_t_kernel(tc, trans, weight, bias, out):
         open_banks = {}
 
         def load_x(t):
-            xr = xraw.tile([P, 2 * C], BF16, name="xr")
+            xr = late["xraw"].tile([P, 2 * C], BF16, name="xr")
             nc.sync.dma_start(
                 out=xr[:].rearrange("p (a c) -> p a c", a=2),
                 in_=trans[t].rearrange("b h w c -> (b h w) c").rearrange("(a p) c -> p a c", p=P),
@@ -76,7 +82,7 @@ def tile_iwht2layer_pa_t_kernel(tc, trans, weight, bias, out):
                 for u in range(2):
                     q = 2 * a + u
                     nc.tensor.transpose(xt[:, q * P : (q + 1) * P], words[:, a, :, u], ident[:])
-            tg = tgrp.tile([P, 2048], BF16, align_bytes=64, name="tg")
+            tg = late["tgrp"].tile([P, 2048], BF16, align_bytes=64, name="tg")
             nc.scalar.copy(
                 out=tg[:, 0:1024].bitcast(F32).rearrange("p (a r u) -> p a r u", a=2, u=2),
                 in_=xt[:].rearrange("p (a u r) -> p a r u", a=2, u=2),
@@ -136,7 +142,10 @@ def tile_iwht2layer_pa_t_kernel(tc, trans, weight, bias, out):
 
         def mx_round(nt, u):
             for rt in range(2):
-                xn = xpool.tile([P, 4, NH], F32, tag="x", name="xn")
+                if nt == 1 and u < 2:
+                    xn = late["x2"].tile([P, 4, NH], F32, tag="x2", name="xn2")
+                else:
+                    xn = xpool.tile([P, 4, NH], F32, tag="x", name="xn")
                 x_of[(nt, rt, u)] = xn
                 for j in range(4):
                     bank = psum.tile([P, NH], F32, tag="bank", name="bank")
@@ -160,11 +169,10 @@ def tile_iwht2layer_pa_t_kernel(tc, trans, weight, bias, out):
                         hi = x_of[(nt, rt, 2 + e)]
                         if (nt, rt, e) in B_ON_GPSIMD:
                             for j in range(4):
-                                ys = ypool.tile([P, NH], F32, name="ys")
-                                nc.gpsimd.tensor_tensor(out=ys[:], in0=lo[:, j, :], in1=hi[:, j, :], op=ALU.subtract)
-                                store(nt, rt, 2 + e, j, ys[:])
-                                nc.gpsimd.tensor_tensor(out=lo[:, j, :], in0=lo[:, j, :], in1=hi[:, j, :], op=ALU.add)
-                                store(nt, rt, e, j, lo[:, j, :])
+                                g_todo.append((nt, rt, e, j))
+                            if nt == 1:
+                                g_drain(len(g_todo))
+                                st_flush()
                         else:
                             nc.vector.tensor_tensor(out=hi[:], in0=lo[:], in1=hi[:], op=ALU.subtract)
                             for j in range(4):
@@ -174,6 +182,22 @@ def tile_iwht2layer_pa_t_kernel(tc, trans, weight, bias, out):
                             )
                             for j in range(4):
                                 store(nt, rt, e, j, lo[:, j, :])
+
+        def g_drain(n):
+            for nt, rt, e, j in g_todo[:n]:
+                lo = x_of[(nt, rt, e)]
+                hi = x_of[(nt, rt, 2 + e)]
+                ys = ypool.tile([P, NH], F32, name="ys")
+                nc.gpsimd.tensor_tensor(out=ys[:], in0=lo[:, j, :], in1=hi[:, j, :], op=ALU.subtract)
+                nc.gpsimd.tensor_tensor(out=lo[:, j, :], in0=lo[:, j, :], in1=hi[:, j, :], op=ALU.add)
+                st_todo.append((nt, rt, 2 + e, j, ys[:]))
+                st_todo.append((nt, rt, e, j, lo[:, j, :]))
+            g_todo[:n] = []
+
+        def st_flush():
+            for nt, rt, i, j, ap in st_todo:
+                store(nt, rt, i, j, ap)
+            st_todo[:] = []
 
         def r8_open(nt, rt):
             for e in range(2):
@@ -207,9 +231,7 @@ def tile_iwht2layer_pa_t_kernel(tc, trans, weight, bias, out):
                 for v in range(4):
                     load_x(4 * k + v)
             if k == 1:
-                nc.sync.dma_start(
-                    out=bias_bc[:], in_=bias.rearrange("a b c k -> (a b c k)").partition_broadcast(P)
-                )
+                nc.sync.dma_start(out=brow[0:1, :], in_=bias.rearrange("a b c k -> (a b c) k"))
             if k < 8:
                 for v in range(4):
                     load_w(rounds[k][0], 4 * rounds[k][1] + v)
@@ -222,13 +244,10 @@ def tile_iwht2layer_pa_t_kernel(tc, trans, weight, bias, out):
                 for v in range(4):
                     prep_w(rounds[k][0], 4 * rounds[k][1] + v)
 
-        for k in range(LOOKAHEAD + 1):
-            loads(k)
-        for k in range(LOOKAHEAD):
-            prep(k)
-        for k in range(8):
+        def body(k):
             nt, u = rounds[k]
             loads(k + LOOKAHEAD + 1)
+            st_flush()
             prep(k + LOOKAHEAD)
             if nt in R8_HALVES and u == 2:
                 r8_open(nt, 0)
@@ -236,3 +255,24 @@ def tile_iwht2layer_pa_t_kernel(tc, trans, weight, bias, out):
                 r8_finish(nt)
             else:
                 mx_round(nt, u)
+            g_drain(G_DRAIN[k])
+
+        with tc.tile_pool(name="xraw", bufs=8) as xraw, tc.tile_pool(name="tgrp", bufs=4) as tgrp:
+            late["xraw"] = xraw
+            late["tgrp"] = tgrp
+            for k in range(LOOKAHEAD + 1):
+                loads(k)
+            for k in range(LOOKAHEAD):
+                prep(k)
+            for h in range(2):
+                pb = psum.tile([P, NH], F32, tag="bank", name="pb")
+                nc.tensor.matmul(out=pb[:], lhsT=ones[:], rhs=brow[:, h * NH : (h + 1) * NH], start=True, stop=True)
+                nc.scalar.copy(out=bias_bc[:, h * NH : (h + 1) * NH], in_=pb[:])
+            for k in range(4 - LOOKAHEAD):
+                body(k)
+        with tc.tile_pool(name="x2", bufs=4) as x2:
+            late["x2"] = x2
+            for k in range(4 - LOOKAHEAD, 8):
+                body(k)
+            g_drain(len(g_todo))
+            st_flush()

@@ -21,22 +21,21 @@ FLOPS = 2 * 16 * 256 * 512 * 1024
 H4 = ((1, 1, 1, 1), (1, -1, 1, -1), (1, 1, -1, -1), (1, -1, -1, 1))
 SCALE = 1.0 / 16.0
 
-R_ON_VECTOR = ((0, 1), (0, 3), (0, 9), (1, 3), (1, 9))
+R_ON_VECTOR = ((0, 1), (0, 3))
 R8_HALVES = ()
-B_ON_GPSIMD = ((0, 0, 0), (0, 0, 1), (0, 1, 0), (0, 1, 1), (1, 0, 1))
-LOOKAHEAD = 1
-G_DRAIN = (0, 0, 0, 4, 4, 4, 4, 0)
 
 
 def tile_iwht2layer_pa_t_kernel(tc, trans, weight, bias, out):
     nc = tc.nc
     with ExitStack() as ctx:
         const = ctx.enter_context(tc.tile_pool(name="const", bufs=1))
+        xraw = ctx.enter_context(tc.tile_pool(name="xraw", bufs=6))
+        tgrp = ctx.enter_context(tc.tile_pool(name="tgrp", bufs=3))
         wraw = ctx.enter_context(tc.tile_pool(name="wraw", bufs=6))
         wgrp = ctx.enter_context(tc.tile_pool(name="wgrp", bufs=3))
         wcod = ctx.enter_context(tc.tile_pool(name="wcod", bufs=3))
-        xpool = ctx.enter_context(tc.tile_pool(name="xpool", bufs=9))
-        ypool = ctx.enter_context(tc.tile_pool(name="ypool", bufs=6))
+        xpool = ctx.enter_context(tc.tile_pool(name="xpool", bufs=12))
+        ypool = ctx.enter_context(tc.tile_pool(name="ypool", bufs=2))
         psum = ctx.enter_context(tc.psum_pool(name="psum", bufs=8))
 
         ident = const.tile([P, P], F32, name="ident")
@@ -44,14 +43,12 @@ def tile_iwht2layer_pa_t_kernel(tc, trans, weight, bias, out):
         bias_bc = const.tile([P, K], F32, name="bias_bc")
         ones = const.tile([P, P], BF16, name="ones")
         brow = const.tile([P, K], BF16, name="brow")
-        nc.vector.memset(ones[:], 1.0)
         nc.vector.memset(brow[:], 0.0)
+        nc.sync.dma_start(out=brow[0:1, :], in_=bias.rearrange("a b c k -> (a b c) k"))
+        nc.vector.memset(ones[:], 1.0)
         tcod = const.tile([P, T, 512], U32, align_bytes=64, name="tcod")
         tsc = const.tile([P, T, 512], U8, align_bytes=64, name="tsc")
 
-        late = {}
-        g_todo = []
-        st_todo = []
         xr_of = {}
         wr_of = {}
         wc_of = {}
@@ -59,7 +56,7 @@ def tile_iwht2layer_pa_t_kernel(tc, trans, weight, bias, out):
         open_banks = {}
 
         def load_x(t):
-            xr = late["xraw"].tile([P, 2 * C], BF16, name="xr")
+            xr = xraw.tile([P, 2 * C], BF16, name="xr")
             nc.sync.dma_start(
                 out=xr[:].rearrange("p (a c) -> p a c", a=2),
                 in_=trans[t].rearrange("b h w c -> (b h w) c").rearrange("(a p) c -> p a c", p=P),
@@ -82,7 +79,7 @@ def tile_iwht2layer_pa_t_kernel(tc, trans, weight, bias, out):
                 for u in range(2):
                     q = 2 * a + u
                     nc.tensor.transpose(xt[:, q * P : (q + 1) * P], words[:, a, :, u], ident[:])
-            tg = late["tgrp"].tile([P, 2048], BF16, align_bytes=64, name="tg")
+            tg = tgrp.tile([P, 2048], BF16, align_bytes=64, name="tg")
             nc.scalar.copy(
                 out=tg[:, 0:1024].bitcast(F32).rearrange("p (a r u) -> p a r u", a=2, u=2),
                 in_=xt[:].rearrange("p (a u r) -> p a r u", a=2, u=2),
@@ -115,7 +112,10 @@ def tile_iwht2layer_pa_t_kernel(tc, trans, weight, bias, out):
         def store(nt, rt, i, j, ap):
             view = out[2 * rt : 2 * rt + 2, :, :, nt * NH : (nt + 1) * NH]
             view = view.rearrange("b (h i) (w j) k -> i j (b h) w k", i=4, j=4)
-            nc.sync.dma_start(out=view[i, j], in_=ap)
+            if nt == 0:
+                nc.gpsimd.dma_start(out=view[i, j], in_=ap)
+            else:
+                nc.sync.dma_start(out=view[i, j], in_=ap)
 
         def butterfly(bank, lo, hi):
             nc.vector.scalar_tensor_tensor(
@@ -142,10 +142,7 @@ def tile_iwht2layer_pa_t_kernel(tc, trans, weight, bias, out):
 
         def mx_round(nt, u):
             for rt in range(2):
-                if nt == 1 and u < 2:
-                    xn = late["x2"].tile([P, 4, NH], F32, tag="x2", name="xn2")
-                else:
-                    xn = xpool.tile([P, 4, NH], F32, tag="x", name="xn")
+                xn = xpool.tile([P, 4, NH], F32, tag="x", name="xn")
                 x_of[(nt, rt, u)] = xn
                 for j in range(4):
                     bank = psum.tile([P, NH], F32, tag="bank", name="bank")
@@ -167,37 +164,13 @@ def tile_iwht2layer_pa_t_kernel(tc, trans, weight, bias, out):
                     for e in range(2):
                         lo = x_of[(nt, rt, e)]
                         hi = x_of[(nt, rt, 2 + e)]
-                        if (nt, rt, e) in B_ON_GPSIMD:
-                            for j in range(4):
-                                g_todo.append((nt, rt, e, j))
-                            if nt == 1:
-                                g_drain(len(g_todo))
-                                st_flush()
-                        else:
-                            nc.vector.tensor_tensor(out=hi[:], in0=lo[:], in1=hi[:], op=ALU.subtract)
-                            for j in range(4):
-                                store(nt, rt, 2 + e, j, hi[:, j, :])
-                            nc.vector.scalar_tensor_tensor(
-                                out=lo[:], in0=lo[:], scalar=2.0, in1=hi[:], op0=ALU.mult, op1=ALU.subtract
-                            )
-                            for j in range(4):
-                                store(nt, rt, e, j, lo[:, j, :])
-
-        def g_drain(n):
-            for nt, rt, e, j in g_todo[:n]:
-                lo = x_of[(nt, rt, e)]
-                hi = x_of[(nt, rt, 2 + e)]
-                ys = ypool.tile([P, NH], F32, name="ys")
-                nc.gpsimd.tensor_tensor(out=ys[:], in0=lo[:, j, :], in1=hi[:, j, :], op=ALU.subtract)
-                nc.gpsimd.tensor_tensor(out=lo[:, j, :], in0=lo[:, j, :], in1=hi[:, j, :], op=ALU.add)
-                st_todo.append((nt, rt, 2 + e, j, ys[:]))
-                st_todo.append((nt, rt, e, j, lo[:, j, :]))
-            g_todo[:n] = []
-
-        def st_flush():
-            for nt, rt, i, j, ap in st_todo:
-                store(nt, rt, i, j, ap)
-            st_todo[:] = []
+                        yd = xpool.tile([P, 4, NH], F32, tag="x", name="yd")
+                        nc.vector.tensor_tensor(out=yd[:], in0=lo[:], in1=hi[:], op=ALU.subtract)
+                        for j in range(4):
+                            store(nt, rt, 2 + e, j, yd[:, j, :])
+                        nc.vector.tensor_tensor(out=lo[:], in0=lo[:], in1=hi[:], op=ALU.add)
+                        for j in range(4):
+                            store(nt, rt, e, j, lo[:, j, :])
 
         def r8_open(nt, rt):
             for e in range(2):
@@ -225,54 +198,38 @@ def tile_iwht2layer_pa_t_kernel(tc, trans, weight, bias, out):
                     r8_close(nt, 1, e, j, bank)
 
         rounds = [(nt, u) for nt in range(2) for u in range(4)]
-
-        def loads(k):
-            if k < 4:
-                for v in range(4):
-                    load_x(4 * k + v)
-            if k == 1:
-                nc.sync.dma_start(out=brow[0:1, :], in_=bias.rearrange("a b c k -> (a b c) k"))
-            if k < 8:
-                for v in range(4):
-                    load_w(rounds[k][0], 4 * rounds[k][1] + v)
-
-        def prep(k):
-            if k < 4:
-                for v in range(4):
-                    prep_x(4 * k + v)
-            if k < 8:
-                for v in range(4):
-                    prep_w(rounds[k][0], 4 * rounds[k][1] + v)
-
-        def body(k):
+        for t in range(4):
+            load_x(t)
+        for t in range(4):
+            load_w(0, t)
+        for t in range(4, 8):
+            load_x(t)
+        for t in range(4):
+            prep_x(t)
+        for h in range(2):
+            pb = psum.tile([P, NH], F32, tag="bank", name="pb")
+            nc.tensor.matmul(out=pb[:], lhsT=ones[:], rhs=brow[:, h * NH : (h + 1) * NH], start=True, stop=True)
+            nc.scalar.copy(out=bias_bc[:, h * NH : (h + 1) * NH], in_=pb[:])
+        for t in range(4):
+            prep_w(0, t)
+        for k in range(8):
             nt, u = rounds[k]
-            loads(k + LOOKAHEAD + 1)
-            st_flush()
-            prep(k + LOOKAHEAD)
+            if k + 1 < 8:
+                nnt, nu = rounds[k + 1]
+                for v in range(4):
+                    load_w(nnt, 4 * nu + v)
+            if k + 2 < 4:
+                for v in range(4):
+                    load_x(4 * (k + 2) + v)
+            if k + 1 < 4:
+                for v in range(4):
+                    prep_x(4 * (k + 1) + v)
+            if k + 1 < 8:
+                for v in range(4):
+                    prep_w(nnt, 4 * nu + v)
             if nt in R8_HALVES and u == 2:
                 r8_open(nt, 0)
             elif nt in R8_HALVES and u == 3:
                 r8_finish(nt)
             else:
                 mx_round(nt, u)
-            g_drain(G_DRAIN[k])
-
-        with tc.tile_pool(name="xraw", bufs=8) as xraw, tc.tile_pool(name="tgrp", bufs=4) as tgrp:
-            late["xraw"] = xraw
-            late["tgrp"] = tgrp
-            for k in range(LOOKAHEAD + 1):
-                loads(k)
-            for k in range(LOOKAHEAD):
-                prep(k)
-            for h in range(2):
-                pb = psum.tile([P, NH], F32, tag="bank", name="pb")
-                nc.tensor.matmul(out=pb[:], lhsT=ones[:], rhs=brow[:, h * NH : (h + 1) * NH], start=True, stop=True)
-                nc.scalar.copy(out=bias_bc[:, h * NH : (h + 1) * NH], in_=pb[:])
-            for k in range(4 - LOOKAHEAD):
-                body(k)
-        with tc.tile_pool(name="x2", bufs=4) as x2:
-            late["x2"] = x2
-            for k in range(4 - LOOKAHEAD, 8):
-                body(k)
-            g_drain(len(g_todo))
-            st_flush()

@@ -9,7 +9,6 @@ F32 = mybir.dt.float32
 U32 = mybir.dt.uint32
 U8 = mybir.dt.uint8
 ALU = mybir.AluOpType
-ACT = mybir.ActivationFunctionType
 
 P = 128
 T = 16
@@ -18,24 +17,33 @@ K = 1024
 NH = 512
 FLOPS = 2 * 16 * 256 * 512 * 1024
 
-H4 = ((1, 1, 1, 1), (1, -1, 1, -1), (1, 1, -1, -1), (1, -1, -1, 1))
 SCALE = 1.0 / 16.0
 
-R_ON_VECTOR = ((0, 1), (0, 3))
-R8_HALVES = ()
+SPREAD = ((4, 8), (1, 2), (5, 10), (6, 11), (7, 9))
+
+COPY_ON_VECTOR = tuple([(0, t) for t in range(1, T, 2)])
+XCOPY_ON_VECTOR = (3,)
+
+
+def parity(x):
+    return sum([(x >> k) & 1 for k in range(4)]) % 2
+
+
+def coset(a, b, x, y):
+    return [t for t in range(T) if parity(a & t) == x and parity(b & t) == y]
 
 
 def tile_iwht2layer_pa_t_kernel(tc, trans, weight, bias, out):
     nc = tc.nc
     with ExitStack() as ctx:
         const = ctx.enter_context(tc.tile_pool(name="const", bufs=1))
-        xraw = ctx.enter_context(tc.tile_pool(name="xraw", bufs=6))
-        tgrp = ctx.enter_context(tc.tile_pool(name="tgrp", bufs=3))
-        wraw = ctx.enter_context(tc.tile_pool(name="wraw", bufs=6))
+        xraw = ctx.enter_context(tc.tile_pool(name="xraw", bufs=8))
+        tgrp = ctx.enter_context(tc.tile_pool(name="tgrp", bufs=2))
+        wraw = ctx.enter_context(tc.tile_pool(name="wraw", bufs=8))
         wgrp = ctx.enter_context(tc.tile_pool(name="wgrp", bufs=3))
-        wcod = ctx.enter_context(tc.tile_pool(name="wcod", bufs=3))
-        xpool = ctx.enter_context(tc.tile_pool(name="xpool", bufs=12))
-        ypool = ctx.enter_context(tc.tile_pool(name="ypool", bufs=2))
+        wcod = ctx.enter_context(tc.tile_pool(name="wcod", bufs=16))
+        rpool = ctx.enter_context(tc.tile_pool(name="rpool", bufs=4))
+        ypool = ctx.enter_context(tc.tile_pool(name="ypool", bufs=14))
         psum = ctx.enter_context(tc.psum_pool(name="psum", bufs=8))
 
         ident = const.tile([P, P], F32, name="ident")
@@ -46,14 +54,13 @@ def tile_iwht2layer_pa_t_kernel(tc, trans, weight, bias, out):
         nc.vector.memset(brow[:], 0.0)
         nc.sync.dma_start(out=brow[0:1, :], in_=bias.rearrange("a b c k -> (a b c) k"))
         nc.vector.memset(ones[:], 1.0)
-        tcod = const.tile([P, T, 512], U32, align_bytes=64, name="tcod")
-        tsc = const.tile([P, T, 512], U8, align_bytes=64, name="tsc")
 
         xr_of = {}
         wr_of = {}
+        wg_of = {}
         wc_of = {}
-        x_of = {}
-        open_banks = {}
+        tc_of = {}
+        sum_of = {}
 
         def load_x(t):
             xr = xraw.tile([P, 2 * C], BF16, name="xr")
@@ -63,173 +70,158 @@ def tile_iwht2layer_pa_t_kernel(tc, trans, weight, bias, out):
             )
             xr_of[t] = xr
 
-        def load_w(nt, t):
+        def load_w(h, t):
             wr = wraw.tile([P, 4 * NH], BF16, name="wr")
             nc.sync.dma_start(
                 out=wr[:].rearrange("p (j n) -> p j n", j=4),
-                in_=weight[t].rearrange("(p j) n -> p j n", j=4)[:, :, nt * NH : (nt + 1) * NH],
+                in_=weight[t].rearrange("(p j) n -> p j n", j=4)[:, :, h * NH : (h + 1) * NH],
             )
-            wr_of[(nt, t)] = wr
+            wr_of[(h, t)] = wr
 
-        def prep_x(t):
-            xr = xr_of[t]
-            words = xr[:].bitcast(F32).rearrange("p (a w u) -> p a w u", a=2, u=2)
-            xt = psum.tile([P, NH], F32, tag="bank", name="xt")
-            for a in range(2):
-                for u in range(2):
-                    q = 2 * a + u
-                    nc.tensor.transpose(xt[:, q * P : (q + 1) * P], words[:, a, :, u], ident[:])
-            tg = tgrp.tile([P, 2048], BF16, align_bytes=64, name="tg")
-            nc.scalar.copy(
-                out=tg[:, 0:1024].bitcast(F32).rearrange("p (a r u) -> p a r u", a=2, u=2),
-                in_=xt[:].rearrange("p (a u r) -> p a r u", a=2, u=2),
+        def prep_x(u):
+            tg = tgrp.tile([P, 4096], BF16, align_bytes=64, name="tg")
+            for v in range(4):
+                words = xr_of[4 * u + v][:].bitcast(F32).rearrange("p (a w e) -> p a w e", a=2, e=2)
+                xt = psum.tile([P, NH], F32, tag="bank", name="xt")
+                for a in range(2):
+                    for e in range(2):
+                        q = 2 * a + e
+                        nc.tensor.transpose(xt[:, q * P : (q + 1) * P], words[:, a, :, e], ident[:])
+                dst = tg[:, v * 1024 : (v + 1) * 1024].bitcast(F32).rearrange("p (a r e) -> p a r e", a=2, e=2)
+                src = xt[:].rearrange("p (a e r) -> p a r e", a=2, e=2)
+                if v in XCOPY_ON_VECTOR:
+                    nc.vector.tensor_copy(out=dst, in_=src)
+                else:
+                    nc.scalar.copy(out=dst, in_=src)
+            tcd = const.tile([P, 4, 256], U32, align_bytes=64, name="tcod%d" % u)
+            tsc = const.tile([P, 4, 256], U8, align_bytes=64, name="tsc%d" % u)
+            tc_of[u] = (tcd, tsc)
+            nc.vector.quantize_mx(
+                out=tcd[:].rearrange("p v r -> p (v r)").bitcast(FP8X4),
+                scales=tsc[:].rearrange("p v r -> p (v r)"),
+                in_=tg[:],
             )
-            if t % 4 == 0 and not (t == 12 and len(R8_HALVES) > 0):
-                nc.vector.quantize_mx(
-                    out=tcod[:, t, 0:256].bitcast(FP8X4), scales=tsc[:, t, 0:256], in_=tg[:, 0:1024]
+
+        def copy_w(h, k):
+            wg = wgrp.tile([P, 4096], BF16, align_bytes=64, name="wg")
+            wg_of[(h, k)] = wg
+            for e in range(2):
+                t = 2 * k + e
+                dst = wg[:, e * 2048 : (e + 1) * 2048].rearrange("p (c i t) -> p c t i", i=4, t=4)
+                src = wr_of[(h, t)][:].rearrange("p (t c i) -> p c t i", t=4, i=4)
+                if (h, t) in COPY_ON_VECTOR:
+                    nc.vector.tensor_copy(out=dst, in_=src)
+                else:
+                    nc.scalar.copy(out=dst, in_=src)
+
+        def quant_w(h, k):
+            wc = wcod.tile([P, 2, NH], U32, align_bytes=64, name="wc")
+            ws = wcod.tile([P, 2, NH], U8, align_bytes=64, name="ws")
+            wc_of[(h, k)] = (wc, ws)
+            nc.vector.quantize_mx(
+                out=wc[:].rearrange("p e n -> p (e n)").bitcast(FP8X4),
+                scales=ws[:].rearrange("p e n -> p (e n)"),
+                in_=wg_of[(h, k)][:],
+            )
+
+        def passes(bank, h, rt, ts, first, last):
+            for n, t in enumerate(ts):
+                tcd, tsc = tc_of[t // 4]
+                wc, ws = wc_of[(h, t // 2)]
+                nc.tensor.matmul_mx(
+                    out=bank[:],
+                    lhsT=tcd[:, t % 4, rt * P : (rt + 1) * P].bitcast(FP8X4),
+                    lhsT_scale=tsc[:, t % 4, rt * P : (rt + 1) * P],
+                    rhs=wc[:, t % 2, :].bitcast(FP8X4),
+                    rhs_scale=ws[:, t % 2, :],
+                    start=(first and n == 0),
+                    stop=(last and n == len(ts) - 1),
                 )
-            else:
-                nc.vector.tensor_scalar_mul(out=tg[:, 1024:2048], in0=tg[:, 0:1024], scalar1=-1.0)
-                nc.vector.quantize_mx(out=tcod[:, t, :].bitcast(FP8X4), scales=tsc[:, t, :], in_=tg[:])
 
-        def prep_w(nt, t):
-            u, v = divmod(t, 4)
-            if v == 0:
-                wc = wcod.tile([P, 4, NH], U32, align_bytes=64, name="wc")
-                ws = wcod.tile([P, 4, NH], U8, align_bytes=64, name="ws")
-                wc_of[(nt, u)] = (wc, ws)
-            wc, ws = wc_of[(nt, u)]
-            wr = wr_of[(nt, t)]
-            wg = wgrp.tile([P, 4 * NH], BF16, align_bytes=64, name="wg")
-            dst = wg[:].rearrange("p (c i t) -> p c t i", i=4, t=4)
-            src = wr[:].rearrange("p (t c i) -> p c t i", t=4, i=4)
-            if (nt, t) in R_ON_VECTOR:
-                nc.vector.tensor_copy(out=dst, in_=src)
-            else:
-                nc.scalar.copy(out=dst, in_=src)
-            nc.vector.quantize_mx(out=wc[:, v, :].bitcast(FP8X4), scales=ws[:, v, :], in_=wg[:])
-
-        def store(nt, rt, i, j, ap):
-            view = out[2 * rt : 2 * rt + 2, :, :, nt * NH : (nt + 1) * NH]
+        def store(h, rt, a, ap):
+            i, j = divmod(a, 4)
+            view = out[2 * rt : 2 * rt + 2, :, :, h * NH : (h + 1) * NH]
             view = view.rearrange("b (h i) (w j) k -> i j (b h) w k", i=4, j=4)
-            if nt == 0:
+            if h == 0:
                 nc.gpsimd.dma_start(out=view[i, j], in_=ap)
             else:
                 nc.sync.dma_start(out=view[i, j], in_=ap)
 
-        def butterfly(bank, lo, hi):
+        def less(dst, bank, src):
             nc.vector.scalar_tensor_tensor(
-                out=hi, in0=bank[:], scalar=-SCALE, in1=lo, op0=ALU.mult, op1=ALU.add
-            )
-            nc.vector.scalar_tensor_tensor(
-                out=lo, in0=bank[:], scalar=SCALE, in1=lo, op0=ALU.mult, op1=ALU.add
+                out=dst, in0=bank[:], scalar=-2.0 * SCALE, in1=src, op0=ALU.mult, op1=ALU.add
             )
 
-        def passes(bank, nt, u, rt, j, flip, start, stop):
-            wc, ws = wc_of[(nt, u)]
-            for v in range(4):
-                t = 4 * u + v
-                col = (0 if H4[j][v] * flip > 0 else 256) + rt * P
-                nc.tensor.matmul_mx(
-                    out=bank[:],
-                    lhsT=tcod[:, t, col : col + P].bitcast(FP8X4),
-                    lhsT_scale=tsc[:, t, col : col + P],
-                    rhs=wc[:, v, :].bitcast(FP8X4),
-                    rhs_scale=ws[:, v, :],
-                    start=(start and v == 0),
-                    stop=(stop and v == 3),
-                )
-
-        def mx_round(nt, u):
+        def all_sum(h, ts, first, last):
             for rt in range(2):
-                xn = xpool.tile([P, 4, NH], F32, tag="x", name="xn")
-                x_of[(nt, rt, u)] = xn
-                for j in range(4):
-                    bank = psum.tile([P, NH], F32, tag="bank", name="bank")
-                    passes(bank, nt, u, rt, j, 1, True, True)
-                    if u == 0:
-                        nc.vector.scalar_tensor_tensor(
-                            out=xn[:, j, :],
-                            in0=bank[:],
-                            scalar=SCALE,
-                            in1=bias_bc[:, nt * NH : (nt + 1) * NH],
-                            op0=ALU.mult,
-                            op1=ALU.add,
-                        )
-                    elif u == 2:
-                        nc.scalar.activation(out=xn[:, j, :], in_=bank[:], func=ACT.Copy, scale=SCALE)
-                    else:
-                        butterfly(bank, x_of[(nt, rt, u - 1)][:, j, :], xn[:, j, :])
-                if u == 3:
-                    for e in range(2):
-                        lo = x_of[(nt, rt, e)]
-                        hi = x_of[(nt, rt, 2 + e)]
-                        yd = xpool.tile([P, 4, NH], F32, tag="x", name="yd")
-                        nc.vector.tensor_tensor(out=yd[:], in0=lo[:], in1=hi[:], op=ALU.subtract)
-                        for j in range(4):
-                            store(nt, rt, 2 + e, j, yd[:, j, :])
-                        nc.vector.tensor_tensor(out=lo[:], in0=lo[:], in1=hi[:], op=ALU.add)
-                        for j in range(4):
-                            store(nt, rt, e, j, lo[:, j, :])
+                if first:
+                    sum_of[(h, rt)] = psum.tile([P, NH], F32, tag="bank", name="ysum")
+                passes(sum_of[(h, rt)], h, rt, ts, first, last)
 
-        def r8_open(nt, rt):
-            for e in range(2):
-                for j in range(4):
-                    bank = psum.tile([P, NH], F32, tag="bank", name="bank")
-                    open_banks[(e, j)] = bank
-                    passes(bank, nt, 2, rt, j, 1, True, False)
+        def root(h, rt):
+            y0 = rpool.tile([P, NH], F32, name="y0")
+            nc.vector.scalar_tensor_tensor(
+                out=y0[:],
+                in0=sum_of[(h, rt)][:],
+                scalar=SCALE,
+                in1=bias_bc[:, h * NH : (h + 1) * NH],
+                op0=ALU.mult,
+                op1=ALU.add,
+            )
+            store(h, rt, 0, y0[:])
+            return y0
 
-        def r8_close(nt, rt, e, j, bank):
-            passes(bank, nt, 3, rt, j, 1 - 2 * e, False, True)
-            lo = x_of[(nt, rt, e)]
-            ys = ypool.tile([P, NH], F32, name="ys")
-            butterfly(bank, lo[:, j, :], ys[:])
-            store(nt, rt, 2 + e, j, ys[:])
-            store(nt, rt, e, j, lo[:, j, :])
+        def plane(h, rt, y0, a, b):
+            banks = {}
+            for x, y in ((1, 1), (1, 0), (0, 1)):
+                bank = psum.tile([P, NH], F32, tag="bank", name="bank")
+                passes(bank, h, rt, coset(a, b, x, y), True, True)
+                banks[(x, y)] = bank
+            z = ypool.tile([P, NH], F32, tag="y", name="z")
+            ya = ypool.tile([P, NH], F32, tag="y", name="ya")
+            w = ypool.tile([P, NH], F32, tag="y", name="w")
+            less(z[:], banks[(1, 1)], y0[:])
+            less(ya[:], banks[(1, 0)], z[:])
+            store(h, rt, a, ya[:])
+            less(w[:], banks[(1, 0)], y0[:])
+            less(z[:], banks[(0, 1)], z[:])
+            store(h, rt, b, z[:])
+            less(w[:], banks[(0, 1)], w[:])
+            store(h, rt, a ^ b, w[:])
 
-        def r8_finish(nt):
-            for e in range(2):
-                for j in range(4):
-                    r8_close(nt, 0, e, j, open_banks[(e, j)])
-            for e in range(2):
-                for j in range(4):
-                    bank = psum.tile([P, NH], F32, tag="bank", name="bank")
-                    passes(bank, nt, 2, 1, j, 1, True, False)
-                    r8_close(nt, 1, e, j, bank)
+        for u in range(4):
+            for v in range(4):
+                load_x(4 * u + v)
+            for v in range(4):
+                load_w(0, 4 * u + v)
+        for t in range(T):
+            load_w(1, t)
 
-        rounds = [(nt, u) for nt in range(2) for u in range(4)]
-        for t in range(4):
-            load_x(t)
-        for t in range(4):
-            load_w(0, t)
-        for t in range(4, 8):
-            load_x(t)
-        for t in range(4):
-            prep_x(t)
+        for u in range(4):
+            prep_x(u)
+            if u == 0:
+                for h in range(2):
+                    pb = psum.tile([P, NH], F32, tag="bank", name="pb")
+                    nc.tensor.matmul(
+                        out=pb[:], lhsT=ones[:], rhs=brow[:, h * NH : (h + 1) * NH], start=True, stop=True
+                    )
+                    nc.scalar.copy(out=bias_bc[:, h * NH : (h + 1) * NH], in_=pb[:])
+            copy_w(0, 2 * u)
+            copy_w(0, 2 * u + 1)
+            quant_w(0, 2 * u)
+            quant_w(0, 2 * u + 1)
+            all_sum(0, [4 * u + v for v in range(4)], u == 0, u == 3)
+
+        copy_w(1, 0)
         for h in range(2):
-            pb = psum.tile([P, NH], F32, tag="bank", name="pb")
-            nc.tensor.matmul(out=pb[:], lhsT=ones[:], rhs=brow[:, h * NH : (h + 1) * NH], start=True, stop=True)
-            nc.scalar.copy(out=bias_bc[:, h * NH : (h + 1) * NH], in_=pb[:])
-        for t in range(4):
-            prep_w(0, t)
-        for k in range(8):
-            nt, u = rounds[k]
-            if k + 1 < 8:
-                nnt, nu = rounds[k + 1]
-                for v in range(4):
-                    load_w(nnt, 4 * nu + v)
-            if k + 2 < 4:
-                for v in range(4):
-                    load_x(4 * (k + 2) + v)
-            if k + 1 < 4:
-                for v in range(4):
-                    prep_x(4 * (k + 1) + v)
-            if k + 1 < 8:
-                for v in range(4):
-                    prep_w(nnt, 4 * nu + v)
-            if nt in R8_HALVES and u == 2:
-                r8_open(nt, 0)
-            elif nt in R8_HALVES and u == 3:
-                r8_finish(nt)
-            else:
-                mx_round(nt, u)
+            step = 0
+            roots = [root(h, rt) for rt in range(2)]
+            for rt in range(2):
+                for a, b in SPREAD:
+                    plane(h, rt, roots[rt], a, b)
+                    if h == 0 and step < 8:
+                        if step + 1 < 8:
+                            copy_w(1, step + 1)
+                        quant_w(1, step)
+                        all_sum(1, [2 * step, 2 * step + 1], step == 0, step == 7)
+                    step += 1

@@ -9,6 +9,7 @@ F32 = mybir.dt.float32
 U32 = mybir.dt.uint32
 U8 = mybir.dt.uint8
 ALU = mybir.AluOpType
+ACT = mybir.ActivationFunctionType
 
 P = 128
 T = 16
@@ -18,6 +19,7 @@ NH = 512
 FLOPS = 2 * 16 * 256 * 512 * 1024
 
 SCALE = 1.0 / 16.0
+WRAW = 10
 
 SPREAD = ((4, 8), (1, 2), (5, 10), (6, 11), (7, 9))
 
@@ -37,14 +39,13 @@ def tile_iwht2layer_pa_t_kernel(tc, trans, weight, bias, out):
     nc = tc.nc
     with ExitStack() as ctx:
         const = ctx.enter_context(tc.tile_pool(name="const", bufs=1))
-        xraw = ctx.enter_context(tc.tile_pool(name="xraw", bufs=8))
-        tgrp = ctx.enter_context(tc.tile_pool(name="tgrp", bufs=2))
-        wraw = ctx.enter_context(tc.tile_pool(name="wraw", bufs=8))
+        wraw = ctx.enter_context(tc.tile_pool(name="wraw", bufs=WRAW))
         wgrp = ctx.enter_context(tc.tile_pool(name="wgrp", bufs=3))
         wcod = ctx.enter_context(tc.tile_pool(name="wcod", bufs=16))
         rpool = ctx.enter_context(tc.tile_pool(name="rpool", bufs=4))
-        ypool = ctx.enter_context(tc.tile_pool(name="ypool", bufs=14))
+        xpool = ctx.enter_context(tc.tile_pool(name="xpool", bufs=8))
         psum = ctx.enter_context(tc.psum_pool(name="psum", bufs=8))
+        pools = {}
 
         ident = const.tile([P, P], F32, name="ident")
         make_identity(nc, ident[:])
@@ -60,10 +61,10 @@ def tile_iwht2layer_pa_t_kernel(tc, trans, weight, bias, out):
         wg_of = {}
         wc_of = {}
         tc_of = {}
-        sum_of = {}
+        x_of = {}
 
         def load_x(t):
-            xr = xraw.tile([P, 2 * C], BF16, name="xr")
+            xr = pools["xraw"].tile([P, 2 * C], BF16, name="xr")
             nc.sync.dma_start(
                 out=xr[:].rearrange("p (a c) -> p a c", a=2),
                 in_=trans[t].rearrange("b h w c -> (b h w) c").rearrange("(a p) c -> p a c", p=P),
@@ -79,7 +80,7 @@ def tile_iwht2layer_pa_t_kernel(tc, trans, weight, bias, out):
             wr_of[(h, t)] = wr
 
         def prep_x(u):
-            tg = tgrp.tile([P, 4096], BF16, align_bytes=64, name="tg")
+            tg = pools["tgrp"].tile([P, 4096], BF16, align_bytes=64, name="tg")
             for v in range(4):
                 words = xr_of[4 * u + v][:].bitcast(F32).rearrange("p (a w e) -> p a w e", a=2, e=2)
                 xt = psum.tile([P, NH], F32, tag="bank", name="xt")
@@ -113,6 +114,10 @@ def tile_iwht2layer_pa_t_kernel(tc, trans, weight, bias, out):
                     nc.vector.tensor_copy(out=dst, in_=src)
                 else:
                     nc.scalar.copy(out=dst, in_=src)
+            for e in range(2):
+                nxt = T * h + 2 * k + e + WRAW
+                if nxt < 2 * T:
+                    load_w(nxt // T, nxt % T)
 
         def quant_w(h, k):
             wc = wcod.tile([P, 2, NH], U32, align_bytes=64, name="wc")
@@ -142,33 +147,40 @@ def tile_iwht2layer_pa_t_kernel(tc, trans, weight, bias, out):
             i, j = divmod(a, 4)
             view = out[2 * rt : 2 * rt + 2, :, :, h * NH : (h + 1) * NH]
             view = view.rearrange("b (h i) (w j) k -> i j (b h) w k", i=4, j=4)
-            if h == 0:
-                nc.gpsimd.dma_start(out=view[i, j], in_=ap)
-            else:
-                nc.sync.dma_start(out=view[i, j], in_=ap)
+            nc.sync.dma_start(out=view[i, j], in_=ap)
 
         def less(dst, bank, src):
             nc.vector.scalar_tensor_tensor(
                 out=dst, in0=bank[:], scalar=-2.0 * SCALE, in1=src, op0=ALU.mult, op1=ALU.add
             )
 
-        def all_sum(h, ts, first, last):
-            for rt in range(2):
-                if first:
-                    sum_of[(h, rt)] = psum.tile([P, NH], F32, tag="bank", name="ysum")
-                passes(sum_of[(h, rt)], h, rt, ts, first, last)
+        def axpy(dst, bank, factor, src):
+            nc.vector.scalar_tensor_tensor(out=dst, in0=bank[:], scalar=factor, in1=src, op0=ALU.mult, op1=ALU.add)
 
-        def root(h, rt):
+        def first_plane_round(h, u):
+            for rt in range(2):
+                bank = psum.tile([P, NH], F32, tag="bank", name="bank")
+                passes(bank, h, rt, [4 * u + v for v in range(4)], True, True)
+                xn = xpool.tile([P, NH], F32, tag="x", name="xn")
+                x_of[(h, rt, u)] = xn
+                if u == 0:
+                    axpy(xn[:], bank, SCALE, bias_bc[:, h * NH : (h + 1) * NH])
+                elif u == 2:
+                    nc.scalar.activation(out=xn[:], in_=bank[:], func=ACT.Copy, scale=SCALE)
+                else:
+                    lo = x_of[(h, rt, u - 1)]
+                    axpy(xn[:], bank, -SCALE, lo[:])
+                    axpy(lo[:], bank, SCALE, lo[:])
+
+        def first_plane_end(h, rt):
+            x0, x1, x2, x3 = [x_of[(h, rt, u)] for u in range(4)]
             y0 = rpool.tile([P, NH], F32, name="y0")
-            nc.vector.scalar_tensor_tensor(
-                out=y0[:],
-                in0=sum_of[(h, rt)][:],
-                scalar=SCALE,
-                in1=bias_bc[:, h * NH : (h + 1) * NH],
-                op0=ALU.mult,
-                op1=ALU.add,
-            )
+            nc.gpsimd.tensor_tensor(out=y0[:], in0=x0[:], in1=x2[:], op=ALU.add)
             store(h, rt, 0, y0[:])
+            for a, lo, hi, op in ((8, x0, x2, ALU.subtract), (4, x1, x3, ALU.add), (12, x1, x3, ALU.subtract)):
+                ya = pools["ypool"].tile([P, NH], F32, tag="y", name="ya")
+                nc.gpsimd.tensor_tensor(out=ya[:], in0=lo[:], in1=hi[:], op=op)
+                store(h, rt, a, ya[:])
             return y0
 
         def plane(h, rt, y0, a, b):
@@ -177,51 +189,61 @@ def tile_iwht2layer_pa_t_kernel(tc, trans, weight, bias, out):
                 bank = psum.tile([P, NH], F32, tag="bank", name="bank")
                 passes(bank, h, rt, coset(a, b, x, y), True, True)
                 banks[(x, y)] = bank
-            z = ypool.tile([P, NH], F32, tag="y", name="z")
-            ya = ypool.tile([P, NH], F32, tag="y", name="ya")
-            w = ypool.tile([P, NH], F32, tag="y", name="w")
+            z = pools["ypool"].tile([P, NH], F32, tag="y", name="z")
+            ya = pools["ypool"].tile([P, NH], F32, tag="y", name="ya")
+            w = pools["ypool"].tile([P, NH], F32, tag="y", name="w")
             less(z[:], banks[(1, 1)], y0[:])
             less(ya[:], banks[(1, 0)], z[:])
             store(h, rt, a, ya[:])
             less(w[:], banks[(1, 0)], y0[:])
+            e = pools["ypool"].tile([P, NH], F32, tag="y", name="e")
+            nc.scalar.activation(out=e[:], in_=banks[(0, 1)][:], func=ACT.Copy, scale=-2.0 * SCALE)
             less(z[:], banks[(0, 1)], z[:])
             store(h, rt, b, z[:])
-            less(w[:], banks[(0, 1)], w[:])
+            nc.gpsimd.tensor_tensor(out=w[:], in0=w[:], in1=e[:], op=ALU.add)
             store(h, rt, a ^ b, w[:])
 
-        for u in range(4):
-            for v in range(4):
-                load_x(4 * u + v)
-            for v in range(4):
-                load_w(0, 4 * u + v)
-        for t in range(T):
-            load_w(1, t)
+        with ExitStack() as head:
+            pools["xraw"] = head.enter_context(tc.tile_pool(name="xraw", bufs=8))
+            pools["tgrp"] = head.enter_context(tc.tile_pool(name="tgrp", bufs=2))
+            for u in range(2):
+                for v in range(4):
+                    load_x(4 * u + v)
+                for v in range(4):
+                    load_w(0, 4 * u + v)
+            for t in range(8, WRAW):
+                load_w(0, t)
 
-        for u in range(4):
-            prep_x(u)
-            if u == 0:
-                for h in range(2):
-                    pb = psum.tile([P, NH], F32, tag="bank", name="pb")
-                    nc.tensor.matmul(
-                        out=pb[:], lhsT=ones[:], rhs=brow[:, h * NH : (h + 1) * NH], start=True, stop=True
-                    )
-                    nc.scalar.copy(out=bias_bc[:, h * NH : (h + 1) * NH], in_=pb[:])
-            copy_w(0, 2 * u)
-            copy_w(0, 2 * u + 1)
-            quant_w(0, 2 * u)
-            quant_w(0, 2 * u + 1)
-            all_sum(0, [4 * u + v for v in range(4)], u == 0, u == 3)
+            for u in range(4):
+                prep_x(u)
+                if u + 2 < 4:
+                    for v in range(4):
+                        load_x(4 * (u + 2) + v)
+                if u == 0:
+                    for h in range(2):
+                        pb = psum.tile([P, NH], F32, tag="bank", name="pb")
+                        nc.tensor.matmul(
+                            out=pb[:], lhsT=ones[:], rhs=brow[:, h * NH : (h + 1) * NH], start=True, stop=True
+                        )
+                        nc.scalar.copy(out=bias_bc[:, h * NH : (h + 1) * NH], in_=pb[:])
+                copy_w(0, 2 * u)
+                copy_w(0, 2 * u + 1)
+                quant_w(0, 2 * u)
+                quant_w(0, 2 * u + 1)
+                first_plane_round(0, u)
 
+        pools["ypool"] = ctx.enter_context(tc.tile_pool(name="ypool", bufs=16))
         copy_w(1, 0)
         for h in range(2):
             step = 0
-            roots = [root(h, rt) for rt in range(2)]
+            roots = [first_plane_end(h, rt) for rt in range(2)]
             for rt in range(2):
-                for a, b in SPREAD:
+                for a, b in SPREAD[1:]:
                     plane(h, rt, roots[rt], a, b)
-                    if h == 0 and step < 8:
+                    if h == 0:
                         if step + 1 < 8:
                             copy_w(1, step + 1)
                         quant_w(1, step)
-                        all_sum(1, [2 * step, 2 * step + 1], step == 0, step == 7)
+                        if step % 2 == 1:
+                            first_plane_round(1, step // 2)
                     step += 1

@@ -16,14 +16,15 @@ T = 16
 C = 512
 K = 1024
 NH = 512
+NQ = 256
 FLOPS = 2 * 16 * 256 * 512 * 1024
 
 SCALE = 1.0 / 16.0
-WRAW = 10
 
 SPREAD = ((4, 8), (1, 2), (5, 10), (6, 11), (7, 9))
 
-COPY_ON_VECTOR = tuple([(0, t) for t in range(1, T, 2)])
+MODES = ("R", "Q")
+COPY_ON_VECTOR = (tuple(range(1, T, 2)), (), ())
 XCOPY_ON_VECTOR = (3,)
 
 
@@ -39,9 +40,9 @@ def tile_iwht2layer_pa_t_kernel(tc, trans, weight, bias, out):
     nc = tc.nc
     with ExitStack() as ctx:
         const = ctx.enter_context(tc.tile_pool(name="const", bufs=1))
-        wraw = ctx.enter_context(tc.tile_pool(name="wraw", bufs=WRAW))
+        wraw = ctx.enter_context(tc.tile_pool(name="wraw", bufs=16))
         wgrp = ctx.enter_context(tc.tile_pool(name="wgrp", bufs=3))
-        wcod = ctx.enter_context(tc.tile_pool(name="wcod", bufs=16))
+        wcod = ctx.enter_context(tc.tile_pool(name="wcod", bufs=14))
         rpool = ctx.enter_context(tc.tile_pool(name="rpool", bufs=4))
         xpool = ctx.enter_context(tc.tile_pool(name="xpool", bufs=8))
         psum = ctx.enter_context(tc.psum_pool(name="psum", bufs=8))
@@ -62,6 +63,16 @@ def tile_iwht2layer_pa_t_kernel(tc, trans, weight, bias, out):
         wc_of = {}
         tc_of = {}
         x_of = {}
+
+        ranges = []
+        units = []
+        for h in range(2):
+            if MODES[h] == "R":
+                ranges.append(("R", h, 0))
+                units.extend([(("R", h, 0), rt) for rt in range(2)])
+            else:
+                ranges.extend([("Q", h, q) for q in range(2)])
+                units.extend([(("Q", h, q), None) for q in range(2)])
 
         def load_x(t):
             xr = pools["xraw"].tile([P, 2 * C], BF16, name="xr")
@@ -103,122 +114,141 @@ def tile_iwht2layer_pa_t_kernel(tc, trans, weight, bias, out):
                 in_=tg[:],
             )
 
-        def copy_w(h, k):
-            wg = wgrp.tile([P, 4096], BF16, align_bytes=64, name="wg")
-            wg_of[(h, k)] = wg
-            for e in range(2):
-                t = 2 * k + e
-                dst = wg[:, e * 2048 : (e + 1) * 2048].rearrange("p (c i t) -> p c t i", i=4, t=4)
-                src = wr_of[(h, t)][:].rearrange("p (t c i) -> p c t i", t=4, i=4)
-                if (h, t) in COPY_ON_VECTOR:
-                    nc.vector.tensor_copy(out=dst, in_=src)
+        def regroup(rng, t, dst, src):
+            dst = dst.rearrange("p (c i t) -> p c t i", i=4, t=4)
+            src = src.rearrange("p t (c i) -> p c t i", i=4)
+            if t in COPY_ON_VECTOR[ranges.index(rng)]:
+                nc.vector.tensor_copy(out=dst, in_=src)
+            else:
+                nc.scalar.copy(out=dst, in_=src)
+
+        def copy_round(rng, u):
+            mode, h, q = rng
+            for g in range(2 if mode == "R" else 1):
+                wg = wgrp.tile([P, 4096], BF16, align_bytes=64, name="wg")
+                wg_of[(rng, u, g)] = wg
+                if mode == "R":
+                    for e in range(2):
+                        t = 4 * u + 2 * g + e
+                        src = wr_of[(h, t)][:].rearrange("p (t n) -> p t n", t=4)
+                        regroup(rng, t, wg[:, e * 2048 : (e + 1) * 2048], src)
                 else:
-                    nc.scalar.copy(out=dst, in_=src)
-            for e in range(2):
-                nxt = T * h + 2 * k + e + WRAW
-                if nxt < 2 * T:
-                    load_w(nxt // T, nxt % T)
+                    for v in range(4):
+                        t = 4 * u + v
+                        src = wr_of[(h, t)][:].rearrange("p (t n) -> p t n", t=4)[:, :, q * NQ : (q + 1) * NQ]
+                        regroup(rng, t, wg[:, v * 1024 : (v + 1) * 1024], src)
 
-        def quant_w(h, k):
-            wc = wcod.tile([P, 2, NH], U32, align_bytes=64, name="wc")
-            ws = wcod.tile([P, 2, NH], U8, align_bytes=64, name="ws")
-            wc_of[(h, k)] = (wc, ws)
-            nc.vector.quantize_mx(
-                out=wc[:].rearrange("p e n -> p (e n)").bitcast(FP8X4),
-                scales=ws[:].rearrange("p e n -> p (e n)"),
-                in_=wg_of[(h, k)][:],
-            )
+        def quant_round(rng, u):
+            for g in range(2 if rng[0] == "R" else 1):
+                wc = wcod.tile([P, 1024], U32, align_bytes=64, name="wc")
+                ws = wcod.tile([P, 1024], U8, align_bytes=64, name="ws")
+                wc_of[(rng, u, g)] = (wc, ws)
+                nc.vector.quantize_mx(out=wc[:].bitcast(FP8X4), scales=ws[:], in_=wg_of[(rng, u, g)][:])
 
-        def passes(bank, h, rt, ts, first, last):
-            for n, t in enumerate(ts):
-                tcd, tsc = tc_of[t // 4]
-                wc, ws = wc_of[(h, t // 2)]
-                nc.tensor.matmul_mx(
-                    out=bank[:],
-                    lhsT=tcd[:, t % 4, rt * P : (rt + 1) * P].bitcast(FP8X4),
-                    lhsT_scale=tsc[:, t % 4, rt * P : (rt + 1) * P],
-                    rhs=wc[:, t % 2, :].bitcast(FP8X4),
-                    rhs_scale=ws[:, t % 2, :],
-                    start=(first and n == 0),
-                    stop=(last and n == len(ts) - 1),
-                )
+        def passes(bank, unit, ts):
+            rng, row = unit
+            if rng[0] == "R":
+                pieces = ((row, 0, NH),)
+            else:
+                pieces = ((0, 0, NQ), (1, NQ, NQ))
+            for rt, lo, width in pieces:
+                for n, t in enumerate(ts):
+                    tcd, tsc = tc_of[t // 4]
+                    if rng[0] == "R":
+                        wc, ws = wc_of[(rng, t // 4, (t % 4) // 2)]
+                        col = (t % 2) * NH
+                    else:
+                        wc, ws = wc_of[(rng, t // 4, 0)]
+                        col = (t % 4) * NQ
+                    nc.tensor.matmul_mx(
+                        out=bank[:, lo : lo + width],
+                        lhsT=tcd[:, t % 4, rt * P : (rt + 1) * P].bitcast(FP8X4),
+                        lhsT_scale=tsc[:, t % 4, rt * P : (rt + 1) * P],
+                        rhs=wc[:, col : col + width].bitcast(FP8X4),
+                        rhs_scale=ws[:, col : col + width],
+                        start=(n == 0),
+                        stop=(n == len(ts) - 1),
+                    )
 
-        def store(h, rt, a, ap):
+        def store(unit, a, tile):
+            (mode, h, q), row = unit
             i, j = divmod(a, 4)
-            view = out[2 * rt : 2 * rt + 2, :, :, h * NH : (h + 1) * NH]
-            view = view.rearrange("b (h i) (w j) k -> i j (b h) w k", i=4, j=4)
-            nc.sync.dma_start(out=view[i, j], in_=ap)
-
-        def less(dst, bank, src):
-            nc.vector.scalar_tensor_tensor(
-                out=dst, in0=bank[:], scalar=-2.0 * SCALE, in1=src, op0=ALU.mult, op1=ALU.add
-            )
+            if mode == "R":
+                pieces = ((row, h * NH, 0, NH),)
+            else:
+                pieces = ((0, h * NH + q * NQ, 0, NQ), (1, h * NH + q * NQ, NQ, NQ))
+            for rt, n0, lo, width in pieces:
+                view = out[2 * rt : 2 * rt + 2, :, :, n0 : n0 + width]
+                view = view.rearrange("b (h i) (w j) k -> i j (b h) w k", i=4, j=4)
+                nc.sync.dma_start(out=view[i, j], in_=tile[:, lo : lo + width])
 
         def axpy(dst, bank, factor, src):
-            nc.vector.scalar_tensor_tensor(out=dst, in0=bank[:], scalar=factor, in1=src, op0=ALU.mult, op1=ALU.add)
+            nc.vector.scalar_tensor_tensor(out=dst, in0=bank, scalar=factor, in1=src, op0=ALU.mult, op1=ALU.add)
 
-        def first_plane_round(h, u):
-            for rt in range(2):
-                bank = psum.tile([P, NH], F32, tag="bank", name="bank")
-                passes(bank, h, rt, [4 * u + v for v in range(4)], True, True)
-                xn = xpool.tile([P, NH], F32, tag="x", name="xn")
-                x_of[(h, rt, u)] = xn
-                if u == 0:
-                    axpy(xn[:], bank, SCALE, bias_bc[:, h * NH : (h + 1) * NH])
-                elif u == 2:
-                    nc.scalar.activation(out=xn[:], in_=bank[:], func=ACT.Copy, scale=SCALE)
-                else:
-                    lo = x_of[(h, rt, u - 1)]
-                    axpy(xn[:], bank, -SCALE, lo[:])
-                    axpy(lo[:], bank, SCALE, lo[:])
+        def first_plane_round(unit, u):
+            (mode, h, q), row = unit
+            bank = psum.tile([P, NH], F32, tag="bank", name="bank")
+            passes(bank, unit, [4 * u + v for v in range(4)])
+            xn = xpool.tile([P, NH], F32, tag="x", name="xn")
+            x_of[(unit, u)] = xn
+            if u == 0 and mode == "R":
+                axpy(xn[:], bank[:], SCALE, bias_bc[:, h * NH : (h + 1) * NH])
+            elif u == 0:
+                n0 = h * NH + q * NQ
+                for rt in range(2):
+                    cols = slice(rt * NQ, (rt + 1) * NQ)
+                    axpy(xn[:, cols], bank[:, cols], SCALE, bias_bc[:, n0 : n0 + NQ])
+            elif u == 2:
+                nc.scalar.activation(out=xn[:], in_=bank[:], func=ACT.Copy, scale=SCALE)
+            else:
+                lo = x_of[(unit, u - 1)]
+                axpy(xn[:], bank[:], -SCALE, lo[:])
+                axpy(lo[:], bank[:], SCALE, lo[:])
 
-        def first_plane_end(h, rt):
-            x0, x1, x2, x3 = [x_of[(h, rt, u)] for u in range(4)]
+        def first_plane_end(unit):
+            x0, x1, x2, x3 = [x_of[(unit, u)] for u in range(4)]
             y0 = rpool.tile([P, NH], F32, name="y0")
             nc.gpsimd.tensor_tensor(out=y0[:], in0=x0[:], in1=x2[:], op=ALU.add)
-            store(h, rt, 0, y0[:])
+            store(unit, 0, y0)
             for a, lo, hi, op in ((8, x0, x2, ALU.subtract), (4, x1, x3, ALU.add), (12, x1, x3, ALU.subtract)):
                 ya = pools["ypool"].tile([P, NH], F32, tag="y", name="ya")
                 nc.gpsimd.tensor_tensor(out=ya[:], in0=lo[:], in1=hi[:], op=op)
-                store(h, rt, a, ya[:])
+                store(unit, a, ya)
             return y0
 
-        def plane(h, rt, y0, a, b):
+        def plane(unit, y0, a, b):
             banks = {}
             for x, y in ((1, 1), (1, 0), (0, 1)):
                 bank = psum.tile([P, NH], F32, tag="bank", name="bank")
-                passes(bank, h, rt, coset(a, b, x, y), True, True)
+                passes(bank, unit, coset(a, b, x, y))
                 banks[(x, y)] = bank
             z = pools["ypool"].tile([P, NH], F32, tag="y", name="z")
             ya = pools["ypool"].tile([P, NH], F32, tag="y", name="ya")
             w = pools["ypool"].tile([P, NH], F32, tag="y", name="w")
-            less(z[:], banks[(1, 1)], y0[:])
-            less(ya[:], banks[(1, 0)], z[:])
-            store(h, rt, a, ya[:])
-            less(w[:], banks[(1, 0)], y0[:])
             e = pools["ypool"].tile([P, NH], F32, tag="y", name="e")
+            axpy(z[:], banks[(1, 1)][:], -2.0 * SCALE, y0[:])
+            axpy(ya[:], banks[(1, 0)][:], -2.0 * SCALE, z[:])
+            store(unit, a, ya)
+            axpy(w[:], banks[(1, 0)][:], -2.0 * SCALE, y0[:])
             nc.scalar.activation(out=e[:], in_=banks[(0, 1)][:], func=ACT.Copy, scale=-2.0 * SCALE)
-            less(z[:], banks[(0, 1)], z[:])
-            store(h, rt, b, z[:])
+            axpy(z[:], banks[(0, 1)][:], -2.0 * SCALE, z[:])
+            store(unit, b, z)
             nc.gpsimd.tensor_tensor(out=w[:], in0=w[:], in1=e[:], op=ALU.add)
-            store(h, rt, a ^ b, w[:])
+            store(unit, a ^ b, w)
 
         with ExitStack() as head:
-            pools["xraw"] = head.enter_context(tc.tile_pool(name="xraw", bufs=8))
+            pools["xraw"] = head.enter_context(tc.tile_pool(name="xraw", bufs=6))
             pools["tgrp"] = head.enter_context(tc.tile_pool(name="tgrp", bufs=2))
-            for u in range(2):
+            for u in range(4):
                 for v in range(4):
                     load_x(4 * u + v)
                 for v in range(4):
                     load_w(0, 4 * u + v)
-            for t in range(8, WRAW):
-                load_w(0, t)
+            for t in range(T):
+                load_w(1, t)
 
             for u in range(4):
                 prep_x(u)
-                if u + 2 < 4:
-                    for v in range(4):
-                        load_x(4 * (u + 2) + v)
                 if u == 0:
                     for h in range(2):
                         pb = psum.tile([P, NH], F32, tag="bank", name="pb")
@@ -226,24 +256,23 @@ def tile_iwht2layer_pa_t_kernel(tc, trans, weight, bias, out):
                             out=pb[:], lhsT=ones[:], rhs=brow[:, h * NH : (h + 1) * NH], start=True, stop=True
                         )
                         nc.scalar.copy(out=bias_bc[:, h * NH : (h + 1) * NH], in_=pb[:])
-                copy_w(0, 2 * u)
-                copy_w(0, 2 * u + 1)
-                quant_w(0, 2 * u)
-                quant_w(0, 2 * u + 1)
-                first_plane_round(0, u)
+                copy_round(ranges[0], u)
+                quant_round(ranges[0], u)
+                first_plane_round(units[0], u)
+                first_plane_round(units[1], u)
 
-        pools["ypool"] = ctx.enter_context(tc.tile_pool(name="ypool", bufs=16))
-        copy_w(1, 0)
-        for h in range(2):
-            step = 0
-            roots = [first_plane_end(h, rt) for rt in range(2)]
-            for rt in range(2):
-                for a, b in SPREAD[1:]:
-                    plane(h, rt, roots[rt], a, b)
-                    if h == 0:
-                        if step + 1 < 8:
-                            copy_w(1, step + 1)
-                        quant_w(1, step)
-                        if step % 2 == 1:
-                            first_plane_round(1, step // 2)
-                    step += 1
+        pools["ypool"] = ctx.enter_context(tc.tile_pool(name="ypool", bufs=14))
+        later = [(rng, u) for rng in ranges[1:] for u in range(4)]
+        copy_round(later[0][0], later[0][1])
+        roots = {0: first_plane_end(units[0]), 1: first_plane_end(units[1])}
+        for k in range(16):
+            n, r = divmod(k, 4)
+            plane(units[n], roots[n], SPREAD[1 + r][0], SPREAD[1 + r][1])
+            if k + 1 < len(later):
+                copy_round(later[k + 1][0], later[k + 1][1])
+            m = k if k < 6 else k - 2
+            if k < 6 or 8 <= k < 10:
+                quant_round(later[m][0], later[m][1])
+                first_plane_round(units[2 + m // 4], m % 4)
+                if m % 4 == 3:
+                    roots[2 + m // 4] = first_plane_end(units[2 + m // 4])

@@ -42,10 +42,11 @@ def tile_iwht2layer_pa_t_kernel(tc, trans, weight, bias, out):
         const = ctx.enter_context(tc.tile_pool(name="const", bufs=1))
         wraw = ctx.enter_context(tc.tile_pool(name="wraw", bufs=16))
         wgrp = ctx.enter_context(tc.tile_pool(name="wgrp", bufs=3))
-        wcod = ctx.enter_context(tc.tile_pool(name="wcod", bufs=14))
+        wcod = ctx.enter_context(tc.tile_pool(name="wcod", bufs=8))
         rpool = ctx.enter_context(tc.tile_pool(name="rpool", bufs=4))
         xpool = ctx.enter_context(tc.tile_pool(name="xpool", bufs=8))
-        psum = ctx.enter_context(tc.psum_pool(name="psum", bufs=8))
+        psum = ctx.enter_context(tc.psum_pool(name="psum", bufs=6))
+        psum2 = ctx.enter_context(tc.psum_pool(name="psum2", bufs=2))
         pools = {}
 
         ident = const.tile([P, P], F32, name="ident")
@@ -53,9 +54,11 @@ def tile_iwht2layer_pa_t_kernel(tc, trans, weight, bias, out):
         bias_bc = const.tile([P, K], F32, name="bias_bc")
         ones = const.tile([P, P], BF16, name="ones")
         brow = const.tile([P, K], BF16, name="brow")
+        bone = const.tile([1, K], BF16, name="bone")
+        nc.sync.dma_start(out=bone[:], in_=bias.rearrange("a b c k -> (a b c) k"))
         nc.vector.memset(brow[:], 0.0)
-        nc.sync.dma_start(out=brow[0:1, :], in_=bias.rearrange("a b c k -> (a b c) k"))
         nc.vector.memset(ones[:], 1.0)
+        nc.vector.tensor_copy(out=brow[0:1, :], in_=bone[:])
 
         xr_of = {}
         wr_of = {}
@@ -140,12 +143,13 @@ def tile_iwht2layer_pa_t_kernel(tc, trans, weight, bias, out):
 
         def quant_round(rng, u):
             for g in range(2 if rng[0] == "R" else 1):
-                wc = wcod.tile([P, 1024], U32, align_bytes=64, name="wc")
-                ws = wcod.tile([P, 1024], U8, align_bytes=64, name="ws")
+                pool = pools["wcod2"] if rng == ranges[1] or (rng == ranges[2] and u < 2) else wcod
+                wc = pool.tile([P, 1024], U32, align_bytes=64, name="wc")
+                ws = pool.tile([P, 1024], U8, align_bytes=64, name="ws")
                 wc_of[(rng, u, g)] = (wc, ws)
                 nc.vector.quantize_mx(out=wc[:].bitcast(FP8X4), scales=ws[:], in_=wg_of[(rng, u, g)][:])
 
-        def passes(bank, unit, ts):
+        def passes(bank, unit, ts, us=(0, 1, 2, 3)):
             rng, row = unit
             if rng[0] == "R":
                 pieces = ((row, 0, NH),)
@@ -153,6 +157,8 @@ def tile_iwht2layer_pa_t_kernel(tc, trans, weight, bias, out):
                 pieces = ((0, 0, NQ), (1, NQ, NQ))
             for rt, lo, width in pieces:
                 for n, t in enumerate(ts):
+                    if t // 4 not in us:
+                        continue
                     tcd, tsc = tc_of[t // 4]
                     if rng[0] == "R":
                         wc, ws = wc_of[(rng, t // 4, (t % 4) // 2)]
@@ -187,7 +193,7 @@ def tile_iwht2layer_pa_t_kernel(tc, trans, weight, bias, out):
 
         def first_plane_round(unit, u):
             (mode, h, q), row = unit
-            bank = psum.tile([P, NH], F32, tag="bank", name="bank")
+            bank = psum2.tile([P, NH], F32, tag="bank", name="bank")
             passes(bank, unit, [4 * u + v for v in range(4)])
             xn = xpool.tile([P, NH], F32, tag="x", name="xn")
             x_of[(unit, u)] = xn
@@ -216,12 +222,21 @@ def tile_iwht2layer_pa_t_kernel(tc, trans, weight, bias, out):
                 store(unit, a, ya)
             return y0
 
+        open_banks = {}
+
+        def plane_passes(unit, a, b, us):
+            for x, y in ((1, 1), (1, 0), (0, 1)):
+                if (unit, a, x, y) not in open_banks:
+                    bank = psum.tile([P, NH], F32, tag="bank", name="bank")
+                    open_banks[(unit, a, x, y)] = bank
+                passes(open_banks[(unit, a, x, y)], unit, coset(a, b, x, y), us)
+
         def plane(unit, y0, a, b):
+            if (unit, a, 1, 1) not in open_banks:
+                plane_passes(unit, a, b, (0, 1, 2, 3))
             banks = {}
             for x, y in ((1, 1), (1, 0), (0, 1)):
-                bank = psum.tile([P, NH], F32, tag="bank", name="bank")
-                passes(bank, unit, coset(a, b, x, y))
-                banks[(x, y)] = bank
+                banks[(x, y)] = open_banks[(unit, a, x, y)]
             z = pools["ypool"].tile([P, NH], F32, tag="y", name="z")
             ya = pools["ypool"].tile([P, NH], F32, tag="y", name="ya")
             w = pools["ypool"].tile([P, NH], F32, tag="y", name="w")
@@ -237,15 +252,13 @@ def tile_iwht2layer_pa_t_kernel(tc, trans, weight, bias, out):
             store(unit, a ^ b, w)
 
         with ExitStack() as head:
-            pools["xraw"] = head.enter_context(tc.tile_pool(name="xraw", bufs=6))
+            pools["xraw"] = head.enter_context(tc.tile_pool(name="xraw", bufs=16))
             pools["tgrp"] = head.enter_context(tc.tile_pool(name="tgrp", bufs=2))
-            for u in range(4):
-                for v in range(4):
-                    load_x(4 * u + v)
-                for v in range(4):
-                    load_w(0, 4 * u + v)
             for t in range(T):
-                load_w(1, t)
+                load_x(t)
+            for h in range(2):
+                for t in range(T):
+                    load_w(h, t)
 
             for u in range(4):
                 prep_x(u)
@@ -256,11 +269,15 @@ def tile_iwht2layer_pa_t_kernel(tc, trans, weight, bias, out):
                             out=pb[:], lhsT=ones[:], rhs=brow[:, h * NH : (h + 1) * NH], start=True, stop=True
                         )
                         nc.scalar.copy(out=bias_bc[:, h * NH : (h + 1) * NH], in_=pb[:])
+            for u in range(4):
                 copy_round(ranges[0], u)
                 quant_round(ranges[0], u)
                 first_plane_round(units[0], u)
                 first_plane_round(units[1], u)
+                for r in range(2):
+                    plane_passes(units[0], SPREAD[1 + r][0], SPREAD[1 + r][1], (u,))
 
+        pools["wcod2"] = ctx.enter_context(tc.tile_pool(name="wcod2", bufs=6))
         pools["ypool"] = ctx.enter_context(tc.tile_pool(name="ypool", bufs=14))
         later = [(rng, u) for rng in ranges[1:] for u in range(4)]
         copy_round(later[0][0], later[0][1])

@@ -23,8 +23,8 @@ SCALE = 1.0 / 16.0
 
 SPREAD = ((4, 8), (1, 2), (5, 10), (6, 11), (7, 9))
 
-MODES = ("R", "Q")
-COPY_ON_VECTOR = (tuple(range(1, T, 2)), (), ())
+MODES = ("R", "R")
+COPY_ON_VECTOR = (tuple(range(1, T, 2)), ())
 XCOPY_ON_VECTOR = (3,)
 
 
@@ -40,7 +40,7 @@ def tile_iwht2layer_pa_t_kernel(tc, trans, weight, bias, out):
     nc = tc.nc
     with ExitStack() as ctx:
         const = ctx.enter_context(tc.tile_pool(name="const", bufs=1))
-        wraw = ctx.enter_context(tc.tile_pool(name="wraw", bufs=16))
+        wraw = ctx.enter_context(tc.tile_pool(name="wraw", bufs=12))
         wgrp = ctx.enter_context(tc.tile_pool(name="wgrp", bufs=3))
         wcod = ctx.enter_context(tc.tile_pool(name="wcod", bufs=8))
         rpool = ctx.enter_context(tc.tile_pool(name="rpool", bufs=4))
@@ -80,10 +80,10 @@ def tile_iwht2layer_pa_t_kernel(tc, trans, weight, bias, out):
         def load_x(t):
             xr = pools["xraw"].tile([P, 2 * C], BF16, name="xr")
             nc.sync.dma_start(
-                out=xr[:].rearrange("p (a c) -> p a c", a=2),
-                in_=trans[t].rearrange("b h w c -> (b h w) c").rearrange("(a p) c -> p a c", p=P),
+                out=xr[:],
+                in_=trans[t].rearrange("b h w c -> (b h w) c").rearrange("(p a) c -> p (a c)", a=2),
             )
-            xr_of[t] = xr
+            xr_of[t] = xr[:]
 
         def load_w(h, t):
             wr = wraw.tile([P, 4 * NH], BF16, name="wr")
@@ -96,7 +96,7 @@ def tile_iwht2layer_pa_t_kernel(tc, trans, weight, bias, out):
         def prep_x(u):
             tg = pools["tgrp"].tile([P, 4096], BF16, align_bytes=64, name="tg")
             for v in range(4):
-                words = xr_of[4 * u + v][:].bitcast(F32).rearrange("p (a w e) -> p a w e", a=2, e=2)
+                words = xr_of[4 * u + v].bitcast(F32).rearrange("p (a w e) -> p a w e", a=2, e=2)
                 xt = psum.tile([P, NH], F32, tag="bank", name="xt")
                 for a in range(2):
                     for e in range(2):
@@ -125,9 +125,9 @@ def tile_iwht2layer_pa_t_kernel(tc, trans, weight, bias, out):
             else:
                 nc.scalar.copy(out=dst, in_=src)
 
-        def copy_round(rng, u):
+        def copy_round(rng, u, gs=(0, 1)):
             mode, h, q = rng
-            for g in range(2 if mode == "R" else 1):
+            for g in gs:
                 wg = wgrp.tile([P, 4096], BF16, align_bytes=64, name="wg")
                 wg_of[(rng, u, g)] = wg
                 if mode == "R":
@@ -141,9 +141,9 @@ def tile_iwht2layer_pa_t_kernel(tc, trans, weight, bias, out):
                         src = wr_of[(h, t)][:].rearrange("p (t n) -> p t n", t=4)[:, :, q * NQ : (q + 1) * NQ]
                         regroup(rng, t, wg[:, v * 1024 : (v + 1) * 1024], src)
 
-        def quant_round(rng, u):
-            for g in range(2 if rng[0] == "R" else 1):
-                pool = pools["wcod2"] if rng == ranges[1] or (rng == ranges[2] and u < 2) else wcod
+        def quant_round(rng, u, gs=(0, 1)):
+            for g in gs:
+                pool = pools["wcod2"] if rng == ranges[1] else wcod
                 wc = pool.tile([P, 1024], U32, align_bytes=64, name="wc")
                 ws = pool.tile([P, 1024], U8, align_bytes=64, name="ws")
                 wc_of[(rng, u, g)] = (wc, ws)
@@ -184,9 +184,9 @@ def tile_iwht2layer_pa_t_kernel(tc, trans, weight, bias, out):
             else:
                 pieces = ((0, h * NH + q * NQ, 0, NQ), (1, h * NH + q * NQ, NQ, NQ))
             for rt, n0, lo, width in pieces:
-                view = out[2 * rt : 2 * rt + 2, :, :, n0 : n0 + width]
-                view = view.rearrange("b (h i) (w j) k -> i j (b h) w k", i=4, j=4)
-                nc.sync.dma_start(out=view[i, j], in_=tile[:, lo : lo + width])
+                view = out[:, :, :, n0 : n0 + width]
+                view = view.rearrange("b (h i) (w2 a j) k -> i j a (b h) w2 k", i=4, a=2, j=4)
+                nc.sync.dma_start(out=view[i, j, rt], in_=tile[:, lo : lo + width])
 
         def axpy(dst, bank, factor, src):
             nc.vector.scalar_tensor_tensor(out=dst, in0=bank, scalar=factor, in1=src, op0=ALU.mult, op1=ALU.add)
@@ -277,19 +277,23 @@ def tile_iwht2layer_pa_t_kernel(tc, trans, weight, bias, out):
                 for r in range(2):
                     plane_passes(units[0], SPREAD[1 + r][0], SPREAD[1 + r][1], (u,))
 
-        pools["wcod2"] = ctx.enter_context(tc.tile_pool(name="wcod2", bufs=6))
-        pools["ypool"] = ctx.enter_context(tc.tile_pool(name="ypool", bufs=14))
-        later = [(rng, u) for rng in ranges[1:] for u in range(4)]
-        copy_round(later[0][0], later[0][1])
+        pools["wcod2"] = ctx.enter_context(tc.tile_pool(name="wcod2", bufs=8))
+        pools["ypool"] = ctx.enter_context(tc.tile_pool(name="ypool", bufs=17))
+        later = [(u, g) for u in range(4) for g in range(2)]
+        copy_round(ranges[1], 0, (0,))
         roots = {0: first_plane_end(units[0]), 1: first_plane_end(units[1])}
+        copy_round(ranges[1], 0, (1,))
+        quant_round(ranges[1], 0, (0,))
         for k in range(16):
             n, r = divmod(k, 4)
             plane(units[n], roots[n], SPREAD[1 + r][0], SPREAD[1 + r][1])
+            if k + 2 < len(later):
+                copy_round(ranges[1], later[k + 2][0], (later[k + 2][1],))
             if k + 1 < len(later):
-                copy_round(later[k + 1][0], later[k + 1][1])
-            m = k if k < 6 else k - 2
-            if k < 6 or 8 <= k < 10:
-                quant_round(later[m][0], later[m][1])
-                first_plane_round(units[2 + m // 4], m % 4)
-                if m % 4 == 3:
-                    roots[2 + m // 4] = first_plane_end(units[2 + m // 4])
+                u, g = later[k + 1]
+                quant_round(ranges[1], u, (g,))
+                if g == 1:
+                    for n2 in (2, 3):
+                        first_plane_round(units[n2], u)
+                        if u == 3:
+                            roots[n2] = first_plane_end(units[n2])

@@ -24,7 +24,7 @@ SCALE = 1.0 / 16.0
 SPREAD = ((4, 8), (1, 2), (5, 10), (6, 11), (7, 9))
 
 MODES = ("R", "R")
-COPY_ON_VECTOR = (tuple(range(1, T, 2)), ())
+COPY_ON_VECTOR = (tuple(range(1, T, 2)), (3, 7, 11, 15))
 XCOPY_ON_VECTOR = (3,)
 
 

@@ -45,8 +45,13 @@ def tile_iwht2layer_pa_t_kernel(tc, trans, weight, bias, out):
         wcod = ctx.enter_context(tc.tile_pool(name="wcod", bufs=8))
         rpool = ctx.enter_context(tc.tile_pool(name="rpool", bufs=4))
         xpool = ctx.enter_context(tc.tile_pool(name="xpool", bufs=8))
-        psum = ctx.enter_context(tc.psum_pool(name="psum", bufs=6))
-        psum2 = ctx.enter_context(tc.psum_pool(name="psum2", bufs=2))
+        psum = ctx.enter_context(tc.psum_pool(name="psum", bufs=1))
+        turn = [0]
+
+        def next_bank():
+            turn[0] += 1
+            return "b%d" % ((turn[0] - 1) % 8)
+
         pools = {}
 
         ident = const.tile([P, P], F32, name="ident")
@@ -97,7 +102,7 @@ def tile_iwht2layer_pa_t_kernel(tc, trans, weight, bias, out):
             tg = pools["tgrp"].tile([P, 4096], BF16, align_bytes=64, name="tg")
             for v in range(4):
                 words = xr_of[4 * u + v].bitcast(F32).rearrange("p (a w e) -> p a w e", a=2, e=2)
-                xt = psum.tile([P, NH], F32, tag="bank", name="xt")
+                xt = psum.tile([P, NH], F32, tag=next_bank(), name="xt")
                 for a in range(2):
                     for e in range(2):
                         q = 2 * a + e
@@ -193,7 +198,7 @@ def tile_iwht2layer_pa_t_kernel(tc, trans, weight, bias, out):
 
         def first_plane_round(unit, u):
             (mode, h, q), row = unit
-            bank = psum2.tile([P, NH], F32, tag="bank", name="bank")
+            bank = psum.tile([P, NH], F32, tag=("b%d" % (6 + row)) if h == 0 else next_bank(), name="bank")
             passes(bank, unit, [4 * u + v for v in range(4)])
             xn = xpool.tile([P, NH], F32, tag="x", name="xn")
             x_of[(unit, u)] = xn
@@ -211,15 +216,22 @@ def tile_iwht2layer_pa_t_kernel(tc, trans, weight, bias, out):
                 axpy(xn[:], bank[:], -SCALE, lo[:])
                 axpy(lo[:], bank[:], SCALE, lo[:])
 
-        def first_plane_end(unit):
-            x0, x1, x2, x3 = [x_of[(unit, u)] for u in range(4)]
+        def first_plane_root(unit):
             y0 = rpool.tile([P, NH], F32, name="y0")
-            nc.gpsimd.tensor_tensor(out=y0[:], in0=x0[:], in1=x2[:], op=ALU.add)
+            nc.gpsimd.tensor_tensor(out=y0[:], in0=x_of[(unit, 0)][:], in1=x_of[(unit, 2)][:], op=ALU.add)
             store(unit, 0, y0)
-            for a, lo, hi, op in ((8, x0, x2, ALU.subtract), (4, x1, x3, ALU.add), (12, x1, x3, ALU.subtract)):
-                ya = pools["ypool"].tile([P, NH], F32, tag="y", name="ya")
-                nc.gpsimd.tensor_tensor(out=ya[:], in0=lo[:], in1=hi[:], op=op)
-                store(unit, a, ya)
+            return y0
+
+        def first_plane_rest(unit, n):
+            a, lo, hi, op = ((8, 0, 2, ALU.subtract), (4, 1, 3, ALU.add), (12, 1, 3, ALU.subtract))[n]
+            ya = pools["ypool"].tile([P, NH], F32, tag="y", name="ya")
+            nc.gpsimd.tensor_tensor(out=ya[:], in0=x_of[(unit, lo)][:], in1=x_of[(unit, hi)][:], op=op)
+            store(unit, a, ya)
+
+        def first_plane_end(unit):
+            y0 = first_plane_root(unit)
+            for n in range(3):
+                first_plane_rest(unit, n)
             return y0
 
         open_banks = {}
@@ -227,7 +239,7 @@ def tile_iwht2layer_pa_t_kernel(tc, trans, weight, bias, out):
         def plane_passes(unit, a, b, us):
             for x, y in ((1, 1), (1, 0), (0, 1)):
                 if (unit, a, x, y) not in open_banks:
-                    bank = psum.tile([P, NH], F32, tag="bank", name="bank")
+                    bank = psum.tile([P, NH], F32, tag=next_bank(), name="bank")
                     open_banks[(unit, a, x, y)] = bank
                 passes(open_banks[(unit, a, x, y)], unit, coset(a, b, x, y), us)
 
@@ -264,11 +276,12 @@ def tile_iwht2layer_pa_t_kernel(tc, trans, weight, bias, out):
                 prep_x(u)
                 if u == 0:
                     for h in range(2):
-                        pb = psum.tile([P, NH], F32, tag="bank", name="pb")
+                        pb = psum.tile([P, NH], F32, tag=next_bank(), name="pb")
                         nc.tensor.matmul(
                             out=pb[:], lhsT=ones[:], rhs=brow[:, h * NH : (h + 1) * NH], start=True, stop=True
                         )
                         nc.scalar.copy(out=bias_bc[:, h * NH : (h + 1) * NH], in_=pb[:])
+            turn[0] = 0
             for u in range(4):
                 copy_round(ranges[0], u)
                 quant_round(ranges[0], u)
@@ -287,6 +300,8 @@ def tile_iwht2layer_pa_t_kernel(tc, trans, weight, bias, out):
         for k in range(16):
             n, r = divmod(k, 4)
             plane(units[n], roots[n], SPREAD[1 + r][0], SPREAD[1 + r][1])
+            if 7 <= k < 13:
+                first_plane_rest(units[2 + (k - 7) // 3], (k - 7) % 3)
             if k + 2 < len(later):
                 copy_round(ranges[1], later[k + 2][0], (later[k + 2][1],))
             if k + 1 < len(later):
@@ -296,4 +311,4 @@ def tile_iwht2layer_pa_t_kernel(tc, trans, weight, bias, out):
                     for n2 in (2, 3):
                         first_plane_round(units[n2], u)
                         if u == 3:
-                            roots[n2] = first_plane_end(units[n2])
+                            roots[n2] = first_plane_root(units[n2])

from contextlib import ExitStack

import concourse.mybir as mybir
from concourse.masks import make_identity

FP8X4 = mybir.dt.float8_e4m3fn_x4
BF16 = mybir.dt.bfloat16
F32 = mybir.dt.float32
U32 = mybir.dt.uint32
U8 = mybir.dt.uint8
ALU = mybir.AluOpType
ACT = mybir.ActivationFunctionType

P = 128
T = 16
C = 512
K = 1024
NH = 512
NQ = 256
FLOPS = 2 * 16 * 256 * 512 * 1024

SCALE = 1.0 / 16.0

SPREAD = ((4, 8), (1, 2), (5, 10), (6, 11), (7, 9))

MODES = ("R", "R")
COPY_ON_VECTOR = (tuple(range(1, T, 2)), (3, 7, 11, 15))
XCOPY_ON_VECTOR = (3,)


def parity(x):
    return sum([(x >> k) & 1 for k in range(4)]) % 2


def coset(a, b, x, y):
    return [t for t in range(T) if parity(a & t) == x and parity(b & t) == y]


def tile_iwht2layer_pa_t_kernel(tc, trans, weight, bias, out):
    nc = tc.nc
    with ExitStack() as ctx:
        const = ctx.enter_context(tc.tile_pool(name="const", bufs=1))
        wraw = ctx.enter_context(tc.tile_pool(name="wraw", bufs=12))
        wgrp = ctx.enter_context(tc.tile_pool(name="wgrp", bufs=3))
        wcod = ctx.enter_context(tc.tile_pool(name="wcod", bufs=8))
        rpool = ctx.enter_context(tc.tile_pool(name="rpool", bufs=4))
        xpool = ctx.enter_context(tc.tile_pool(name="xpool", bufs=8))
        psum = ctx.enter_context(tc.psum_pool(name="psum", bufs=1))
        turn = [0]

        def next_bank():
            turn[0] += 1
            return "b%d" % ((turn[0] - 1) % 8)

        pools = {}

        ident = const.tile([P, P], F32, name="ident")
        make_identity(nc, ident[:])
        bias_bc = const.tile([P, K], F32, name="bias_bc")
        ones = const.tile([P, P], BF16, name="ones")
        brow = const.tile([P, K], BF16, name="brow")
        bone = const.tile([1, K], BF16, name="bone")
        nc.sync.dma_start(out=bone[:], in_=bias.rearrange("a b c k -> (a b c) k"))
        nc.vector.memset(brow[:], 0.0)
        nc.vector.memset(ones[:], 1.0)
        nc.vector.tensor_copy(out=brow[0:1, :], in_=bone[:])

        xr_of = {}
        wr_of = {}
        wg_of = {}
        wc_of = {}
        tc_of = {}
        x_of = {}

        ranges = []
        units = []
        for h in range(2):
            if MODES[h] == "R":
                ranges.append(("R", h, 0))
                units.extend([(("R", h, 0), rt) for rt in range(2)])
            else:
                ranges.extend([("Q", h, q) for q in range(2)])
                units.extend([(("Q", h, q), None) for q in range(2)])

        def load_x(t):
            xr = pools["xraw"].tile([P, 2 * C], BF16, name="xr")
            nc.sync.dma_start(
                out=xr[:],
                in_=trans[t].rearrange("b h w c -> (b h w) c").rearrange("(p a) c -> p (a c)", a=2),
            )
            xr_of[t] = xr[:]

        def load_w(h, t):
            wr = wraw.tile([P, 4 * NH], BF16, name="wr")
            nc.sync.dma_start(
                out=wr[:].rearrange("p (j n) -> p j n", j=4),
                in_=weight[t].rearrange("(p j) n -> p j n", j=4)[:, :, h * NH : (h + 1) * NH],
            )
            wr_of[(h, t)] = wr

        def prep_x(u):
            tg = pools["tgrp"].tile([P, 4096], BF16, align_bytes=64, name="tg")
            for v in range(4):
                words = xr_of[4 * u + v].bitcast(F32).rearrange("p (a w e) -> p a w e", a=2, e=2)
                xt = psum.tile([P, NH], F32, tag=next_bank(), name="xt")
                for a in range(2):
                    for e in range(2):
                        q = 2 * a + e
                        nc.tensor.transpose(xt[:, q * P : (q + 1) * P], words[:, a, :, e], ident[:])
                dst = tg[:, v * 1024 : (v + 1) * 1024].bitcast(F32).rearrange("p (a r e) -> p a r e", a=2, e=2)
                src = xt[:].rearrange("p (a e r) -> p a r e", a=2, e=2)
                if v in XCOPY_ON_VECTOR:
                    nc.vector.tensor_copy(out=dst, in_=src)
                else:
                    nc.scalar.copy(out=dst, in_=src)
            tcd = const.tile([P, 4, 256], U32, align_bytes=64, name="tcod%d" % u)
            tsc = const.tile([P, 4, 256], U8, align_bytes=64, name="tsc%d" % u)
            tc_of[u] = (tcd, tsc)
            nc.vector.quantize_mx(
                out=tcd[:].rearrange("p v r -> p (v r)").bitcast(FP8X4),
                scales=tsc[:].rearrange("p v r -> p (v r)"),
                in_=tg[:],
            )

        def regroup(rng, t, dst, src):
            dst = dst.rearrange("p (c i t) -> p c t i", i=4, t=4)
            src = src.rearrange("p t (c i) -> p c t i", i=4)
            if t in COPY_ON_VECTOR[ranges.index(rng)]:
                nc.vector.tensor_copy(out=dst, in_=src)
            else:
                nc.scalar.copy(out=dst, in_=src)

        def copy_round(rng, u, gs=(0, 1)):
            mode, h, q = rng
            for g in gs:
                wg = wgrp.tile([P, 4096], BF16, align_bytes=64, name="wg")
                wg_of[(rng, u, g)] = wg
                if mode == "R":
                    for e in range(2):
                        t = 4 * u + 2 * g + e
                        src = wr_of[(h, t)][:].rearrange("p (t n) -> p t n", t=4)
                        regroup(rng, t, wg[:, e * 2048 : (e + 1) * 2048], src)
                else:
                    for v in range(4):
                        t = 4 * u + v
                        src = wr_of[(h, t)][:].rearrange("p (t n) -> p t n", t=4)[:, :, q * NQ : (q + 1) * NQ]
                        regroup(rng, t, wg[:, v * 1024 : (v + 1) * 1024], src)

        def quant_round(rng, u, gs=(0, 1)):
            for g in gs:
                pool = pools["wcod2"] if rng == ranges[1] else wcod
                wc = pool.tile([P, 1024], U32, align_bytes=64, name="wc")
                ws = pool.tile([P, 1024], U8, align_bytes=64, name="ws")
                wc_of[(rng, u, g)] = (wc, ws)
                nc.vector.quantize_mx(out=wc[:].bitcast(FP8X4), scales=ws[:], in_=wg_of[(rng, u, g)][:])

        def passes(bank, unit, ts, us=(0, 1, 2, 3)):
            rng, row = unit
            if rng[0] == "R":
                pieces = ((row, 0, NH),)
            else:
                pieces = ((0, 0, NQ), (1, NQ, NQ))
            for rt, lo, width in pieces:
                for n, t in enumerate(ts):
                    if t // 4 not in us:
                        continue
                    tcd, tsc = tc_of[t // 4]
                    if rng[0] == "R":
                        wc, ws = wc_of[(rng, t // 4, (t % 4) // 2)]
                        col = (t % 2) * NH
                    else:
                        wc, ws = wc_of[(rng, t // 4, 0)]
                        col = (t % 4) * NQ
                    nc.tensor.matmul_mx(
                        out=bank[:, lo : lo + width],
                        lhsT=tcd[:, t % 4, rt * P : (rt + 1) * P].bitcast(FP8X4),
                        lhsT_scale=tsc[:, t % 4, rt * P : (rt + 1) * P],
                        rhs=wc[:, col : col + width].bitcast(FP8X4),
                        rhs_scale=ws[:, col : col + width],
                        start=(n == 0),
                        stop=(n == len(ts) - 1),
                    )

        def store(unit, a, tile):
            (mode, h, q), row = unit
            i, j = divmod(a, 4)
            if mode == "R":
                pieces = ((row, h * NH, 0, NH),)
            else:
                pieces = ((0, h * NH + q * NQ, 0, NQ), (1, h * NH + q * NQ, NQ, NQ))
            for rt, n0, lo, width in pieces:
                view = out[:, :, :, n0 : n0 + width]
                view = view.rearrange("b (h i) (w2 a j) k -> i j a (b h) w2 k", i=4, a=2, j=4)
                nc.sync.dma_start(out=view[i, j, rt], in_=tile[:, lo : lo + width])

        def axpy(dst, bank, factor, src):
            nc.vector.scalar_tensor_tensor(out=dst, in0=bank, scalar=factor, in1=src, op0=ALU.mult, op1=ALU.add)

        def first_plane_round(unit, u):
            (mode, h, q), row = unit
            bank = psum.tile([P, NH], F32, tag=("b%d" % (6 + row)) if h == 0 else next_bank(), name="bank")
            passes(bank, unit, [4 * u + v for v in range(4)])
            xn = xpool.tile([P, NH], F32, tag="x", name="xn")
            x_of[(unit, u)] = xn
            if u == 0 and mode == "R":
                axpy(xn[:], bank[:], SCALE, bias_bc[:, h * NH : (h + 1) * NH])
            elif u == 0:
                n0 = h * NH + q * NQ
                for rt in range(2):
                    cols = slice(rt * NQ, (rt + 1) * NQ)
                    axpy(xn[:, cols], bank[:, cols], SCALE, bias_bc[:, n0 : n0 + NQ])
            elif u == 2:
                nc.scalar.activation(out=xn[:], in_=bank[:], func=ACT.Copy, scale=SCALE)
            else:
                lo = x_of[(unit, u - 1)]
                axpy(xn[:], bank[:], -SCALE, lo[:])
                axpy(lo[:], bank[:], SCALE, lo[:])

        def first_plane_root(unit):
            y0 = rpool.tile([P, NH], F32, name="y0")
            nc.gpsimd.tensor_tensor(out=y0[:], in0=x_of[(unit, 0)][:], in1=x_of[(unit, 2)][:], op=ALU.add)
            store(unit, 0, y0)
            return y0

        def first_plane_rest(unit, n):
            a, lo, hi, op = ((8, 0, 2, ALU.subtract), (4, 1, 3, ALU.add), (12, 1, 3, ALU.subtract))[n]
            ya = pools["ypool"].tile([P, NH], F32, tag="y", name="ya")
            nc.gpsimd.tensor_tensor(out=ya[:], in0=x_of[(unit, lo)][:], in1=x_of[(unit, hi)][:], op=op)
            store(unit, a, ya)

        def first_plane_end(unit):
            y0 = first_plane_root(unit)
            for n in range(3):
                first_plane_rest(unit, n)
            return y0

        open_banks = {}

        def plane_passes(unit, a, b, us):
            for x, y in ((1, 1), (1, 0), (0, 1)):
                if (unit, a, x, y) not in open_banks:
                    bank = psum.tile([P, NH], F32, tag=next_bank(), name="bank")
                    open_banks[(unit, a, x, y)] = bank
                passes(open_banks[(unit, a, x, y)], unit, coset(a, b, x, y), us)

        def plane(unit, y0, a, b):
            if (unit, a, 1, 1) not in open_banks:
                plane_passes(unit, a, b, (0, 1, 2, 3))
            banks = {}
            for x, y in ((1, 1), (1, 0), (0, 1)):
                banks[(x, y)] = open_banks[(unit, a, x, y)]
            z = pools["ypool"].tile([P, NH], F32, tag="y", name="z")
            ya = pools["ypool"].tile([P, NH], F32, tag="y", name="ya")
            w = pools["ypool"].tile([P, NH], F32, tag="y", name="w")
            e = pools["ypool"].tile([P, NH], F32, tag="y", name="e")
            axpy(z[:], banks[(1, 1)][:], -2.0 * SCALE, y0[:])
            axpy(ya[:], banks[(1, 0)][:], -2.0 * SCALE, z[:])
            store(unit, a, ya)
            axpy(w[:], banks[(1, 0)][:], -2.0 * SCALE, y0[:])
            nc.scalar.activation(out=e[:], in_=banks[(0, 1)][:], func=ACT.Copy, scale=-2.0 * SCALE)
            axpy(z[:], banks[(0, 1)][:], -2.0 * SCALE, z[:])
            store(unit, b, z)
            nc.gpsimd.tensor_tensor(out=w[:], in0=w[:], in1=e[:], op=ALU.add)
            store(unit, a ^ b, w)

        with ExitStack() as head:
            pools["xraw"] = head.enter_context(tc.tile_pool(name="xraw", bufs=16))
            pools["tgrp"] = head.enter_context(tc.tile_pool(name="tgrp", bufs=2))
            for t in range(T):
                load_x(t)
            for h in range(2):
                for t in range(T):
                    load_w(h, t)

            for u in range(4):
                prep_x(u)
                if u == 0:
                    for h in range(2):
                        pb = psum.tile([P, NH], F32, tag=next_bank(), name="pb")
                        nc.tensor.matmul(
                            out=pb[:], lhsT=ones[:], rhs=brow[:, h * NH : (h + 1) * NH], start=True, stop=True
                        )
                        nc.scalar.copy(out=bias_bc[:, h * NH : (h + 1) * NH], in_=pb[:])
            turn[0] = 0
            for u in range(4):
                copy_round(ranges[0], u)
                quant_round(ranges[0], u)
                first_plane_round(units[0], u)
                first_plane_round(units[1], u)
                for r in range(2):
                    plane_passes(units[0], SPREAD[1 + r][0], SPREAD[1 + r][1], (u,))

        pools["wcod2"] = ctx.enter_context(tc.tile_pool(name="wcod2", bufs=8))
        pools["ypool"] = ctx.enter_context(tc.tile_pool(name="ypool", bufs=17))
        later = [(u, g) for u in range(4) for g in range(2)]
        copy_round(ranges[1], 0, (0,))
        roots = {0: first_plane_end(units[0]), 1: first_plane_end(units[1])}
        copy_round(ranges[1], 0, (1,))
        quant_round(ranges[1], 0, (0,))
        for k in range(16):
            n, r = divmod(k, 4)
            plane(units[n], roots[n], SPREAD[1 + r][0], SPREAD[1 + r][1])
            if 7 <= k < 13:
                first_plane_rest(units[2 + (k - 7) // 3], (k - 7) % 3)
            if k + 2 < len(later):
                copy_round(ranges[1], later[k + 2][0], (later[k + 2][1],))
            if k + 1 < len(later):
                u, g = later[k + 1]
                quant_round(ranges[1], u, (g,))
                if g == 1:
                    for n2 in (2, 3):
                        first_plane_round(units[n2], u)
                        if u == 3:
                            roots[n2] = first_plane_root(units[n2])
